import numpy as np
import ml_dtypes


def mxq(x, axis, fmt="e4m3"):
    dtype, down = {"e4m3": (ml_dtypes.float8_e4m3fn, 7), "e5m2": (ml_dtypes.float8_e5m2, 14)}[fmt]
    v = np.moveaxis(np.asarray(x, np.float32).astype(ml_dtypes.bfloat16).astype(np.float64), axis, -1)
    blocks = v.reshape(v.shape[:-1] + (-1, 32))
    amax = np.abs(blocks).max(-1, keepdims=True)
    byte = np.maximum(np.where(amax > 0, np.frexp(amax)[1] - 1 + 127, 0) - down, 1)
    scale = np.exp2(byte - 127.0)
    codes = (blocks / scale).astype(np.float32).astype(dtype).astype(np.float64)
    return np.moveaxis((codes * scale).reshape(v.shape), -1, axis)


WIDE = False


def mx_kscale(k):
    if not WIDE:
        return np.ones(k)
    levels = np.array([10, -10, 5, -5, 0])
    a = np.random.permutation(np.resize(levels, k // 512 * 4)).reshape(k // 512, 4)
    idx = np.arange(k)
    return np.exp2(a[idx // 512, idx % 128 // 32])


BF16 = ml_dtypes.bfloat16


def bf(x):
    return np.asarray(x, np.float32).astype(BF16)


def f64(x):
    return np.asarray(x).astype(np.float64)


B, N, D = 512, 17, 512
LN_EPS = 1e-5
LEAKY_SLOPE = 0.01


def setup_inputs():
    s = mx_kscale(D)
    s = s / s.max()
    return {"h": bf(np.random.standard_normal((B, N, D)) * 0.5 * s),
            "W_l": bf(np.random.standard_normal((D, D)) * 2.0 / np.sqrt(D) / s[None, :]),
            "b_l": bf(np.random.standard_normal(D) * 0.1),
            "W_r": bf(np.random.standard_normal((D, D)) * 1.0 / np.sqrt(D) / s[None, :]),
            "ln_g": bf(1.0 + 0.1 * np.random.standard_normal(D)),
            "ln_b": bf(-0.4 + 0.2 * np.random.standard_normal(D))}


def reference(h, W_l, b_l, W_r, ln_g, ln_b):
    h = f64(h)
    n = h.shape[1]
    mean_neigh = (np.sum(h, axis=1, keepdims=True) - h) / (n - 1)
    c = ((mxq(mean_neigh, 2, "e4m3") @ mxq(f64(W_l), 1, "e4m3").T) + f64(b_l)
         + (mxq(h, 2, "e4m3") @ mxq(f64(W_r), 1, "e4m3").T))
    mu = np.mean(c, axis=-1, keepdims=True)
    var = np.mean(np.square(c - mu), axis=-1, keepdims=True)
    y = (c - mu) * (1.0 / np.sqrt(var + LN_EPS)) * f64(ln_g) + f64(ln_b)
    a = np.where(y > 0, y, LEAKY_SLOPE * y)
    return a + h

@@ -1,0 +1,259 @@
+from contextlib import ExitStack
+
+import concourse.mybir as mybir
+from concourse.masks import make_identity
+
+F32 = mybir.dt.float32
+BF16 = mybir.dt.bfloat16
+U32 = mybir.dt.uint32
+U8 = mybir.dt.uint8
+FP8X4 = mybir.dt.float8_e4m3fn_x4
+ALU = mybir.AluOpType
+ACT = mybir.ActivationFunctionType
+AXIS = mybir.AxisListType
+
+P = 128
+PACK = 4
+HALVES = 2
+GRAPHS = 512
+NODES = 17
+D = 512
+BLOCKS = GRAPHS // P
+OTHERS = NODES - 1
+LAST = NODES - 1
+GRAPHS_PER_SUM = P // OTHERS
+SUMS = P // GRAPHS_PER_SUM
+LN_EPS = 1e-5
+LEAKY_SLOPE = 0.01
+
+FLOPS = 2 * 2 * GRAPHS * NODES * D * D
+
+
+def turn_rows(nc, turned_pool, identity, rows, grouped):
+    words = rows.bitcast(F32)
+    turned = turned_pool.tile([P, HALVES, P], F32)
+    for u in range(HALVES):
+        nc.tensor.transpose(turned[:, u, :], words[:, u * P : (u + 1) * P], identity[:])
+    nc.scalar.copy(out=grouped.bitcast(F32), in_=turned[:].rearrange("p u r -> p r u"))
+
+
+def quantise_weight(nc, stage, turned_pool, identity, weight, codes, scales):
+    rows = stage.tile([P, D // P, D], BF16, name="weight_rows")
+    nc.sync.dma_start(out=rows[:], in_=weight.rearrange("(a p) k -> p a k", p=P))
+    grouped = stage.tile([P, D, PACK], BF16, name="weight_grouped", align_bytes=64)
+    for a in range(D // P):
+        turn_rows(nc, turned_pool, identity, rows[:, a, :], grouped[:, a * P : (a + 1) * P, :])
+    nc.vector.quantize_mx(
+        out=codes[:].bitcast(FP8X4),
+        scales=scales[:],
+        in_=grouped[:].rearrange("p o t -> p (o t)"),
+    )
+
+
+def tile_gnnnicheencoder_pa_t_kernel(tc, h, W_l, b_l, W_r, ln_g, ln_b, out):
+    nc = tc.nc
+    with ExitStack() as stack:
+        const = stack.enter_context(tc.tile_pool(name="const", bufs=1))
+        stage = stack.enter_context(tc.tile_pool(name="stage", bufs=2))
+        blocks = stack.enter_context(tc.tile_pool(name="blocks", bufs=BLOCKS))
+        means = stack.enter_context(tc.tile_pool(name="means", bufs=2))
+        operands = stack.enter_context(tc.tile_pool(name="operands", bufs=4))
+        work = stack.enter_context(tc.tile_pool(name="work", bufs=3))
+        stats = stack.enter_context(tc.tile_pool(name="stats", bufs=6))
+        turned_pool = stack.enter_context(tc.psum_pool(name="turned", bufs=2))
+        sums_pool = stack.enter_context(tc.psum_pool(name="sums", bufs=1))
+        acc_pool = stack.enter_context(tc.psum_pool(name="acc", bufs=3))
+
+        identity = const.tile([P, P], F32)
+        make_identity(nc, identity[:])
+        graph_of_partition = const.tile([P, GRAPHS_PER_SUM], F32)
+        nc.vector.tensor_reduce(
+            out=graph_of_partition[:],
+            in_=identity[:].rearrange("p (g i) -> p g i", i=OTHERS),
+            axis=AXIS.X,
+            op=ALU.add,
+        )
+        node_sum = const.tile([P, GRAPHS_PER_SUM], BF16)
+        nc.vector.tensor_scalar_mul(out=node_sum[:], in0=graph_of_partition[:], scalar1=1.0 / OTHERS)
+        eps = const.tile([P, 1], F32)
+        nc.vector.memset(eps[:], LN_EPS)
+
+        wr_codes = const.tile([P, D], U32, align_bytes=64)
+        wr_scales = const.tile([P, D], U8, align_bytes=64)
+        wl_codes = const.tile([P, D], U32, align_bytes=64)
+        wl_scales = const.tile([P, D], U8, align_bytes=64)
+        quantise_weight(nc, stage, turned_pool, identity, W_r, wr_codes, wr_scales)
+        quantise_weight(nc, stage, turned_pool, identity, W_l, wl_codes, wl_scales)
+
+        bias_rows = const.tile([P, D], BF16)
+        gain_rows = const.tile([P, D], BF16)
+        shift_rows = const.tile([P, D], BF16)
+        nc.sync.dma_start(out=bias_rows[:], in_=b_l.partition_broadcast(P))
+        nc.sync.dma_start(out=gain_rows[:], in_=ln_g.partition_broadcast(P))
+        nc.sync.dma_start(out=shift_rows[:], in_=ln_b.partition_broadcast(P))
+
+        by_graph = []
+        by_node = []
+        for s in range(BLOCKS):
+            block = h[s * P : (s + 1) * P, :, :]
+            nodes_on_partitions = blocks.tile([P, SUMS, D], BF16, name="by_node")
+            spread = block[:, 0:OTHERS, :].rearrange("(T g) i k -> g i T k", g=GRAPHS_PER_SUM)
+            for g in range(GRAPHS_PER_SUM):
+                nc.sync.dma_start(
+                    out=nodes_on_partitions[g * OTHERS : (g + 1) * OTHERS, :, :], in_=spread[g]
+                )
+            graphs_on_partitions = blocks.tile([P, NODES, D], BF16, name="by_graph")
+            nc.sync.dma_start(out=graphs_on_partitions[:], in_=block)
+            by_node.append(nodes_on_partitions)
+            by_graph.append(graphs_on_partitions)
+
+        tiles = [(s, i) for s in range(BLOCKS) for i in [LAST] + list(range(LAST))]
+        grouped_of = {}
+        mean_of = {}
+        codes_of = {}
+        centred_of = {}
+
+        def turn(s, i):
+            grouped = operands.tile([P, 2, P, PACK], BF16, name="grouped", align_bytes=64)
+            turn_rows(nc, turned_pool, identity, by_graph[s][:, i, :], grouped[:, 0, :, :])
+            grouped_of[(s, i)] = grouped
+
+        def block_mean(s):
+            sums = sums_pool.tile([P, PACK, P], F32)
+            for T in range(SUMS):
+                columns = by_node[s][:, T, :].rearrange("p (u q e) -> p u e q", u=HALVES, e=2)
+                for t in range(PACK):
+                    nc.tensor.matmul(
+                        out=sums[:, t, T * GRAPHS_PER_SUM : (T + 1) * GRAPHS_PER_SUM],
+                        lhsT=columns[:, t // 2, t % 2, :],
+                        rhs=node_sum[:],
+                        start=True,
+                        stop=True,
+                    )
+            mean = means.tile([P, P, PACK], F32, name="mean")
+            nc.vector.scalar_tensor_tensor(
+                out=mean[:],
+                in0=grouped_of[(s, LAST)][:, 0, :, :],
+                scalar=1.0 / OTHERS,
+                in1=sums[:].rearrange("p t g -> p g t"),
+                op0=ALU.mult,
+                op1=ALU.add,
+            )
+            mean_of[s] = mean
+
+        def neighbours(s, i):
+            grouped = grouped_of[(s, i)]
+            nc.vector.scalar_tensor_tensor(
+                out=grouped[:, 1, :, :],
+                in0=grouped[:, 0, :, :],
+                scalar=-1.0 / OTHERS,
+                in1=mean_of[s][:],
+                op0=ALU.mult,
+                op1=ALU.add,
+            )
+
+        def quantise(s, i):
+            codes = operands.tile([P, 2, P], U32, name="codes", align_bytes=64)
+            scales = operands.tile([P, 2, P], U8, name="scales", align_bytes=64)
+            nc.vector.quantize_mx(
+                out=codes[:].rearrange("p x r -> p (x r)").bitcast(FP8X4),
+                scales=scales[:].rearrange("p x r -> p (x r)"),
+                in_=grouped_of[(s, i)][:].rearrange("p x r t -> p (x r t)"),
+            )
+            codes_of[(s, i)] = (codes, scales)
+
+        def multiply(s, i):
+            codes, scales = codes_of[(s, i)]
+            acc = acc_pool.tile([P, D], F32)
+            nc.tensor.matmul_mx(
+                out=acc[:],
+                lhsT=codes[:, 0, :].bitcast(FP8X4),
+                lhsT_scale=scales[:, 0, :],
+                rhs=wr_codes[:].bitcast(FP8X4),
+                rhs_scale=wr_scales[:],
+                start=True,
+                stop=False,
+            )
+            nc.tensor.matmul_mx(
+                out=acc[:],
+                lhsT=codes[:, 1, :].bitcast(FP8X4),
+                lhsT_scale=scales[:, 1, :],
+                rhs=wl_codes[:].bitcast(FP8X4),
+                rhs_scale=wl_scales[:],
+                start=False,
+                stop=True,
+            )
+            c = work.tile([P, D], F32, name="c")
+            row_sum = stats.tile([P, 1], F32, name="row_sum")
+            nc.vector.scalar_tensor_tensor(
+                out=c[:],
+                in0=acc[:],
+                scalar=1.0,
+                in1=bias_rows[:],
+                op0=ALU.mult,
+                op1=ALU.add,
+                accum_out=row_sum[:],
+            )
+            minus_mean = stats.tile([P, 1], F32, name="minus_mean")
+            nc.vector.tensor_scalar_mul(out=minus_mean[:], in0=row_sum[:], scalar1=-1.0 / D)
+            squares = work.tile([P, D], BF16, name="squares")
+            square_sum = stats.tile([P, 1], F32, name="square_sum")
+            nc.scalar.activation(
+                out=squares[:],
+                in_=c[:],
+                func=ACT.Square,
+                bias=minus_mean[:],
+                scale=1.0,
+                accum_out=square_sum[:],
+            )
+            deviation = stats.tile([P, 1], F32, name="deviation")
+            nc.scalar.activation(
+                out=deviation[:], in_=square_sum[:], func=ACT.Sqrt, bias=eps[:], scale=1.0 / D
+            )
+            centred_of[(s, i)] = (c, minus_mean, deviation)
+
+        def finish(s, i):
+            c, minus_mean, deviation = centred_of[(s, i)]
+            inverse = stats.tile([P, 1], F32, name="inverse")
+            nc.vector.reciprocal(out=inverse[:], in_=deviation[:])
+            gained = work.tile([P, D], F32, name="gained")
+            nc.vector.scalar_tensor_tensor(
+                out=gained[:],
+                in0=c[:],
+                scalar=minus_mean[:],
+                in1=gain_rows[:],
+                op0=ALU.add,
+                op1=ALU.mult,
+            )
+            y = work.tile([P, D], F32, name="y")
+            nc.vector.scalar_tensor_tensor(
+                out=y[:],
+                in0=gained[:],
+                scalar=inverse[:],
+                in1=shift_rows[:],
+                op0=ALU.mult,
+                op1=ALU.add,
+            )
+            a = work.tile([P, D], F32, name="a")
+            nc.vector.scalar_tensor_tensor(
+                out=a[:], in0=y[:], scalar=LEAKY_SLOPE, in1=y[:], op0=ALU.mult, op1=ALU.max
+            )
+            result = work.tile([P, D], F32, name="result")
+            nc.vector.tensor_add(out=result[:], in0=a[:], in1=by_graph[s][:, i, :])
+            nc.sync.dma_start(out=out[s * P : (s + 1) * P, i, :], in_=result[:])
+
+        count = len(tiles)
+        for step in range(count + 4):
+            if step < count:
+                turn(*tiles[step])
+            if 1 <= step < count + 1:
+                s, i = tiles[step - 1]
+                if i == LAST:
+                    block_mean(s)
+                neighbours(s, i)
+            if 2 <= step < count + 2:
+                quantise(*tiles[step - 2])
+            if 3 <= step < count + 3:
+                multiply(*tiles[step - 3])
+            if 4 <= step:
+                finish(*tiles[step - 4])

@@ -5,6 +5,7 @@ from concourse.masks import make_identity
 
 F32 = mybir.dt.float32
 BF16 = mybir.dt.bfloat16
+I32 = mybir.dt.int32
 U32 = mybir.dt.uint32
 U8 = mybir.dt.uint8
 FP8X4 = mybir.dt.float8_e4m3fn_x4
@@ -18,6 +19,7 @@ HALVES = 2
 GRAPHS = 512
 NODES = 17
 D = 512
+CHUNKS = D // P
 BLOCKS = GRAPHS // P
 OTHERS = NODES - 1
 LAST = NODES - 1
@@ -25,24 +27,30 @@ GRAPHS_PER_SUM = P // OTHERS
 SUMS = P // GRAPHS_PER_SUM
 LN_EPS = 1e-5
 LEAKY_SLOPE = 0.01
+DEPTH = 9
 
 FLOPS = 2 * 2 * GRAPHS * NODES * D * D
 
 
-def turn_rows(nc, turned_pool, identity, rows, grouped):
+def turn_words(nc, turned_pool, identity, rows):
     words = rows.bitcast(F32)
     turned = turned_pool.tile([P, HALVES, P], F32)
     for u in range(HALVES):
         nc.tensor.transpose(turned[:, u, :], words[:, u * P : (u + 1) * P], identity[:])
+    return turned
+
+
+def group_words(nc, turned, grouped):
     nc.scalar.copy(out=grouped.bitcast(F32), in_=turned[:].rearrange("p u r -> p r u"))
 
 
 def quantise_weight(nc, stage, turned_pool, identity, weight, codes, scales):
-    rows = stage.tile([P, D // P, D], BF16, name="weight_rows")
+    rows = stage.tile([P, CHUNKS, D], BF16, name="weight_rows")
     nc.sync.dma_start(out=rows[:], in_=weight.rearrange("(a p) k -> p a k", p=P))
     grouped = stage.tile([P, D, PACK], BF16, name="weight_grouped", align_bytes=64)
-    for a in range(D // P):
-        turn_rows(nc, turned_pool, identity, rows[:, a, :], grouped[:, a * P : (a + 1) * P, :])
+    for a in range(CHUNKS):
+        turned = turn_words(nc, turned_pool, identity, rows[:, a, :])
+        group_words(nc, turned, grouped[:, a * P : (a + 1) * P, :])
     nc.vector.quantize_mx(
         out=codes[:].bitcast(FP8X4),
         scales=scales[:],
@@ -53,16 +61,18 @@ def quantise_weight(nc, stage, turned_pool, identity, weight, codes, scales):
 def tile_gnnnicheencoder_pa_t_kernel(tc, h, W_l, b_l, W_r, ln_g, ln_b, out):
     nc = tc.nc
     with ExitStack() as stack:
+        stack.enter_context(tc.manual_schedule())
         const = stack.enter_context(tc.tile_pool(name="const", bufs=1))
         stage = stack.enter_context(tc.tile_pool(name="stage", bufs=2))
         blocks = stack.enter_context(tc.tile_pool(name="blocks", bufs=BLOCKS))
         means = stack.enter_context(tc.tile_pool(name="means", bufs=2))
-        operands = stack.enter_context(tc.tile_pool(name="operands", bufs=4))
-        work = stack.enter_context(tc.tile_pool(name="work", bufs=3))
-        stats = stack.enter_context(tc.tile_pool(name="stats", bufs=6))
+        work = stack.enter_context(tc.tile_pool(name="work", bufs=4))
+        stats = stack.enter_context(tc.tile_pool(name="stats", bufs=4))
         turned_pool = stack.enter_context(tc.psum_pool(name="turned", bufs=2))
         sums_pool = stack.enter_context(tc.psum_pool(name="sums", bufs=1))
-        acc_pool = stack.enter_context(tc.psum_pool(name="acc", bufs=3))
+        acc_pool = stack.enter_context(tc.psum_pool(name="acc", bufs=2))
+        features_pool = stack.enter_context(tc.psum_pool(name="features", bufs=1))
+        rows_pool = stack.enter_context(tc.psum_pool(name="rows", bufs=2))
 
         identity = const.tile([P, P], F32)
         make_identity(nc, identity[:])
@@ -77,6 +87,8 @@ def tile_gnnnicheencoder_pa_t_kernel(tc, h, W_l, b_l, W_r, ln_g, ln_b, out):
         nc.vector.tensor_scalar_mul(out=node_sum[:], in0=graph_of_partition[:], scalar1=1.0 / OTHERS)
         eps = const.tile([P, 1], F32)
         nc.vector.memset(eps[:], LN_EPS)
+        vector_rows = const.tile([P, P], BF16)
+        nc.vector.memset(vector_rows[:].bitcast(I32), 0)
 
         wr_codes = const.tile([P, D], U32, align_bytes=64)
         wr_scales = const.tile([P, D], U8, align_bytes=64)
@@ -86,15 +98,24 @@ def tile_gnnnicheencoder_pa_t_kernel(tc, h, W_l, b_l, W_r, ln_g, ln_b, out):
         quantise_weight(nc, stage, turned_pool, identity, W_l, wl_codes, wl_scales)
 
         bias_rows = const.tile([P, D], BF16)
-        gain_rows = const.tile([P, D], BF16)
-        shift_rows = const.tile([P, D], BF16)
         nc.sync.dma_start(out=bias_rows[:], in_=b_l.partition_broadcast(P))
-        nc.sync.dma_start(out=gain_rows[:], in_=ln_g.partition_broadcast(P))
-        nc.sync.dma_start(out=shift_rows[:], in_=ln_b.partition_broadcast(P))
+        nc.sync.dma_start(out=vector_rows[0:CHUNKS, :], in_=ln_g.rearrange("(f p) -> f p", p=P))
+        nc.sync.dma_start(
+            out=vector_rows[CHUNKS : 2 * CHUNKS, :], in_=ln_b.rearrange("(f p) -> f p", p=P)
+        )
+        vector_rows_f32 = const.tile([P, P], F32)
+        nc.vector.tensor_copy(out=vector_rows_f32[:], in_=vector_rows[:])
+        turned = turned_pool.tile([P, HALVES, P], F32)
+        nc.tensor.transpose(turned[:, 0, :], vector_rows_f32[:], identity[:])
+        per_feature = const.tile([P, 2 * CHUNKS], F32)
+        nc.vector.tensor_copy(out=per_feature[:], in_=turned[:, 0, 0 : 2 * CHUNKS])
+        gain = per_feature[:, 0:CHUNKS]
+        shift = per_feature[:, CHUNKS : 2 * CHUNKS]
 
         by_graph = []
         by_node = []
-        for s in range(BLOCKS):
+
+        def load_block(s):
             block = h[s * P : (s + 1) * P, :, :]
             nodes_on_partitions = blocks.tile([P, SUMS, D], BF16, name="by_node")
             spread = block[:, 0:OTHERS, :].rearrange("(T g) i k -> g i T k", g=GRAPHS_PER_SUM)
@@ -107,42 +128,52 @@ def tile_gnnnicheencoder_pa_t_kernel(tc, h, W_l, b_l, W_r, ln_g, ln_b, out):
             by_node.append(nodes_on_partitions)
             by_graph.append(graphs_on_partitions)
 
+        load_block(0)
+        load_block(1)
+
         tiles = [(s, i) for s in range(BLOCKS) for i in [LAST] + list(range(LAST))]
-        grouped_of = {}
+        count = len(tiles)
+        sums_of = {}
         mean_of = {}
-        codes_of = {}
-        centred_of = {}
+        kept = {}
 
-        def turn(s, i):
-            grouped = operands.tile([P, 2, P, PACK], BF16, name="grouped", align_bytes=64)
-            turn_rows(nc, turned_pool, identity, by_graph[s][:, i, :], grouped[:, 0, :, :])
-            grouped_of[(s, i)] = grouped
+        def sum_nodes(s, T):
+            if T == 0:
+                sums_of[s] = sums_pool.tile([P, PACK, P], F32, name="sums")
+            columns = by_node[s][:, T, :].rearrange("p (u q e) -> p u e q", u=HALVES, e=2)
+            for t in range(PACK):
+                nc.tensor.matmul(
+                    out=sums_of[s][:, t, T * GRAPHS_PER_SUM : (T + 1) * GRAPHS_PER_SUM],
+                    lhsT=columns[:, t // 2, t % 2, :],
+                    rhs=node_sum[:],
+                    start=True,
+                    stop=True,
+                )
 
-        def block_mean(s):
-            sums = sums_pool.tile([P, PACK, P], F32)
-            for T in range(SUMS):
-                columns = by_node[s][:, T, :].rearrange("p (u q e) -> p u e q", u=HALVES, e=2)
-                for t in range(PACK):
-                    nc.tensor.matmul(
-                        out=sums[:, t, T * GRAPHS_PER_SUM : (T + 1) * GRAPHS_PER_SUM],
-                        lhsT=columns[:, t // 2, t % 2, :],
-                        rhs=node_sum[:],
-                        start=True,
-                        stop=True,
-                    )
+        def block_mean(s, n):
             mean = means.tile([P, P, PACK], F32, name="mean")
             nc.vector.scalar_tensor_tensor(
                 out=mean[:],
-                in0=grouped_of[(s, LAST)][:, 0, :, :],
+                in0=kept[("grouped", n)][:, 0, :, :],
                 scalar=1.0 / OTHERS,
-                in1=sums[:].rearrange("p t g -> p g t"),
+                in1=sums_of[s][:].rearrange("p t g -> p g t"),
                 op0=ALU.mult,
                 op1=ALU.add,
             )
             mean_of[s] = mean
 
-        def neighbours(s, i):
-            grouped = grouped_of[(s, i)]
+        def turn(n):
+            s, i = tiles[n]
+            kept[("turned", n)] = turn_words(nc, turned_pool, identity, by_graph[s][:, i, :])
+
+        def group(n):
+            grouped = work.tile([P, 2, P, PACK], BF16, name="grouped", align_bytes=64)
+            group_words(nc, kept[("turned", n)], grouped[:, 0, :, :])
+            kept[("grouped", n)] = grouped
+
+        def neighbours(n):
+            s, i = tiles[n]
+            grouped = kept[("grouped", n)]
             nc.vector.scalar_tensor_tensor(
                 out=grouped[:, 1, :, :],
                 in0=grouped[:, 0, :, :],
@@ -152,18 +183,18 @@ def tile_gnnnicheencoder_pa_t_kernel(tc, h, W_l, b_l, W_r, ln_g, ln_b, out):
                 op1=ALU.add,
             )
 
-        def quantise(s, i):
-            codes = operands.tile([P, 2, P], U32, name="codes", align_bytes=64)
-            scales = operands.tile([P, 2, P], U8, name="scales", align_bytes=64)
+        def quantise(n):
+            codes = work.tile([P, 2, P], U32, name="codes", align_bytes=64)
+            scales = work.tile([P, 2, P], U8, name="scales", align_bytes=64)
             nc.vector.quantize_mx(
                 out=codes[:].rearrange("p x r -> p (x r)").bitcast(FP8X4),
                 scales=scales[:].rearrange("p x r -> p (x r)"),
-                in_=grouped_of[(s, i)][:].rearrange("p x r t -> p (x r t)"),
+                in_=kept[("grouped", n)][:].rearrange("p x r t -> p (x r t)"),
             )
-            codes_of[(s, i)] = (codes, scales)
+            kept[("codes", n)] = (codes, scales)
 
-        def multiply(s, i):
-            codes, scales = codes_of[(s, i)]
+        def multiply(n):
+            codes, scales = kept[("codes", n)]
             acc = acc_pool.tile([P, D], F32)
             nc.tensor.matmul_mx(
                 out=acc[:],
@@ -183,77 +214,148 @@ def tile_gnnnicheencoder_pa_t_kernel(tc, h, W_l, b_l, W_r, ln_g, ln_b, out):
                 start=False,
                 stop=True,
             )
+            kept[("acc", n)] = acc
+
+        def add_bias(n):
             c = work.tile([P, D], F32, name="c")
             row_sum = stats.tile([P, 1], F32, name="row_sum")
             nc.vector.scalar_tensor_tensor(
                 out=c[:],
-                in0=acc[:],
+                in0=kept[("acc", n)][:],
                 scalar=1.0,
                 in1=bias_rows[:],
                 op0=ALU.mult,
                 op1=ALU.add,
                 accum_out=row_sum[:],
             )
+            kept[("c", n)] = c
+            kept[("row_sum", n)] = row_sum
+
+        def negate_mean(n):
             minus_mean = stats.tile([P, 1], F32, name="minus_mean")
-            nc.vector.tensor_scalar_mul(out=minus_mean[:], in0=row_sum[:], scalar1=-1.0 / D)
+            nc.scalar.mul(out=minus_mean[:], in_=kept[("row_sum", n)][:], mul=-1.0 / D)
+            kept[("minus_mean", n)] = minus_mean
+
+        def sum_squares(n):
             squares = work.tile([P, D], BF16, name="squares")
             square_sum = stats.tile([P, 1], F32, name="square_sum")
             nc.scalar.activation(
                 out=squares[:],
-                in_=c[:],
+                in_=kept[("c", n)][:],
                 func=ACT.Square,
-                bias=minus_mean[:],
+                bias=kept[("minus_mean", n)][:],
                 scale=1.0,
                 accum_out=square_sum[:],
             )
-            deviation = stats.tile([P, 1], F32, name="deviation")
-            nc.scalar.activation(
-                out=deviation[:], in_=square_sum[:], func=ACT.Sqrt, bias=eps[:], scale=1.0 / D
-            )
-            centred_of[(s, i)] = (c, minus_mean, deviation)
+            kept[("square_sum", n)] = square_sum
 
-        def finish(s, i):
-            c, minus_mean, deviation = centred_of[(s, i)]
+        def invert_deviation(n):
             inverse = stats.tile([P, 1], F32, name="inverse")
-            nc.vector.reciprocal(out=inverse[:], in_=deviation[:])
-            gained = work.tile([P, D], F32, name="gained")
-            nc.vector.scalar_tensor_tensor(
-                out=gained[:],
-                in0=c[:],
-                scalar=minus_mean[:],
-                in1=gain_rows[:],
-                op0=ALU.add,
-                op1=ALU.mult,
+            nc.scalar.activation(
+                out=inverse[:],
+                in_=kept[("square_sum", n)][:],
+                func=ACT.Abs_reciprocal_sqrt,
+                bias=eps[:],
+                scale=1.0 / D,
             )
-            y = work.tile([P, D], F32, name="y")
+            kept[("inverse", n)] = inverse
+
+        def fold_mean(n):
+            offset = stats.tile([P, 1], F32, name="offset")
+            nc.scalar.activation(
+                out=offset[:],
+                in_=kept[("minus_mean", n)][:],
+                func=ACT.Copy,
+                scale=kept[("inverse", n)][:],
+            )
+            kept[("offset", n)] = offset
+
+        def normalise(n):
+            normal = work.tile([P, D], F32, name="normal")
+            nc.scalar.activation(
+                out=normal[:],
+                in_=kept[("c", n)][:],
+                func=ACT.Identity,
+                bias=kept[("offset", n)][:],
+                scale=kept[("inverse", n)][:],
+            )
+            kept[("normal", n)] = normal
+
+        def to_features(n):
+            normal = kept[("normal", n)]
+            normal_turned = features_pool.tile([P, CHUNKS, P], F32)
+            for f in range(CHUNKS):
+                nc.tensor.transpose(
+                    normal_turned[:, f, :], normal[:, f * P : (f + 1) * P], identity[:]
+                )
+            kept[("normal_turned", n)] = normal_turned
+
+        def gain_and_shift(n):
+            normal_turned = kept[("normal_turned", n)]
+            y_turned = work.tile([P, CHUNKS, P], F32, name="y_turned")
+            for f in range(CHUNKS):
+                nc.scalar.activation(
+                    out=y_turned[:, f, :],
+                    in_=normal_turned[:, f, :],
+                    func=ACT.Identity,
+                    bias=shift[:, f : f + 1],
+                    scale=gain[:, f : f + 1],
+                )
+            kept[("y_turned", n)] = y_turned
+
+        def leaky_relu(n):
+            y_turned = kept[("y_turned", n)]
+            a_turned = work.tile([P, CHUNKS, P], F32, name="a_turned")
             nc.vector.scalar_tensor_tensor(
-                out=y[:],
-                in0=gained[:],
-                scalar=inverse[:],
-                in1=shift_rows[:],
+                out=a_turned[:],
+                in0=y_turned[:],
+                scalar=LEAKY_SLOPE,
+                in1=y_turned[:],
                 op0=ALU.mult,
-                op1=ALU.add,
+                op1=ALU.max,
             )
-            a = work.tile([P, D], F32, name="a")
-            nc.vector.scalar_tensor_tensor(
-                out=a[:], in0=y[:], scalar=LEAKY_SLOPE, in1=y[:], op0=ALU.mult, op1=ALU.max
-            )
+            kept[("a_turned", n)] = a_turned
+
+        def to_rows(n):
+            a_turned = kept[("a_turned", n)]
+            a_rows = rows_pool.tile([P, D], F32)
+            for f in range(CHUNKS):
+                nc.tensor.transpose(a_rows[:, f * P : (f + 1) * P], a_turned[:, f, :], identity[:])
+            kept[("a_rows", n)] = a_rows
+
+        def add_residual(n):
+            s, i = tiles[n]
             result = work.tile([P, D], F32, name="result")
-            nc.vector.tensor_add(out=result[:], in0=a[:], in1=by_graph[s][:, i, :])
+            nc.vector.tensor_add(out=result[:], in0=kept[("a_rows", n)][:], in1=by_graph[s][:, i, :])
             nc.sync.dma_start(out=out[s * P : (s + 1) * P, i, :], in_=result[:])
 
-        count = len(tiles)
-        for step in range(count + 4):
-            if step < count:
-                turn(*tiles[step])
-            if 1 <= step < count + 1:
-                s, i = tiles[step - 1]
-                if i == LAST:
-                    block_mean(s)
-                neighbours(s, i)
-            if 2 <= step < count + 2:
-                quantise(*tiles[step - 2])
-            if 3 <= step < count + 3:
-                multiply(*tiles[step - 3])
-            if 4 <= step:
-                finish(*tiles[step - 4])
+        def run(stage_of_tile, n):
+            if 0 <= n < count:
+                stage_of_tile(n)
+
+        for T in range(SUMS):
+            sum_nodes(0, T)
+
+        for k in range(count + DEPTH):
+            if k % NODES == 0 and k // NODES + 2 < BLOCKS:
+                load_block(k // NODES + 2)
+            if 0 <= k - 1 < count and tiles[k - 1][1] == LAST:
+                block_mean(tiles[k - 1][0], k - 1)
+            run(multiply, k - 3)
+            run(to_features, k - 7)
+            run(to_rows, k - DEPTH)
+            run(turn, k)
+            if k < count and k % NODES > 0 and k // NODES + 1 < BLOCKS:
+                sum_nodes(k // NODES + 1, k % NODES - 1)
+            run(negate_mean, k - 4)
+            run(normalise, k - 6)
+            run(sum_squares, k - 4)
+            run(gain_and_shift, k - 7)
+            run(invert_deviation, k - 4)
+            run(group, k)
+            run(fold_mean, k - 4)
+            run(neighbours, k - 1)
+            run(quantise, k - 2)
+            run(leaky_relu, k - 8)
+            run(add_bias, k - 3)
+            run(add_residual, k - DEPTH)

@@ -27,30 +27,34 @@ GRAPHS_PER_SUM = P // OTHERS
 SUMS = P // GRAPHS_PER_SUM
 LN_EPS = 1e-5
 LEAKY_SLOPE = 0.01
-DEPTH = 9
+PAIR = 2
+SUMS_PER_STEP = 4
+DEPTH = 8
 
 FLOPS = 2 * 2 * GRAPHS * NODES * D * D
 
 
-def turn_words(nc, turned_pool, identity, rows):
+def turn_words(nc, identity, rows, turned):
     words = rows.bitcast(F32)
-    turned = turned_pool.tile([P, HALVES, P], F32)
     for u in range(HALVES):
         nc.tensor.transpose(turned[:, u, :], words[:, u * P : (u + 1) * P], identity[:])
-    return turned
 
 
 def group_words(nc, turned, grouped):
-    nc.scalar.copy(out=grouped.bitcast(F32), in_=turned[:].rearrange("p u r -> p r u"))
+    nc.scalar.copy(out=grouped.bitcast(F32), in_=turned[:].rearrange("p j u r -> p j r u"))
 
 
 def quantise_weight(nc, stage, turned_pool, identity, weight, codes, scales):
     rows = stage.tile([P, CHUNKS, D], BF16, name="weight_rows")
     nc.sync.dma_start(out=rows[:], in_=weight.rearrange("(a p) k -> p a k", p=P))
     grouped = stage.tile([P, D, PACK], BF16, name="weight_grouped", align_bytes=64)
-    for a in range(CHUNKS):
-        turned = turn_words(nc, turned_pool, identity, rows[:, a, :])
-        group_words(nc, turned, grouped[:, a * P : (a + 1) * P, :])
+    for a in range(0, CHUNKS, PAIR):
+        turned = turned_pool.tile([P, PAIR, HALVES, P], F32)
+        for j in range(PAIR):
+            turn_words(nc, identity, rows[:, a + j, :], turned[:, j, :, :])
+        group_words(
+            nc, turned, grouped[:, a * P : (a + PAIR) * P, :].rearrange("p (j o) t -> p j o t", j=PAIR)
+        )
     nc.vector.quantize_mx(
         out=codes[:].bitcast(FP8X4),
         scales=scales[:],
@@ -66,13 +70,13 @@ def tile_gnnnicheencoder_pa_t_kernel(tc, h, W_l, b_l, W_r, ln_g, ln_b, out):
         stage = stack.enter_context(tc.tile_pool(name="stage", bufs=2))
         blocks = stack.enter_context(tc.tile_pool(name="blocks", bufs=BLOCKS))
         means = stack.enter_context(tc.tile_pool(name="means", bufs=2))
-        work = stack.enter_context(tc.tile_pool(name="work", bufs=4))
+        work = stack.enter_context(tc.tile_pool(name="work", bufs=2))
         stats = stack.enter_context(tc.tile_pool(name="stats", bufs=4))
-        turned_pool = stack.enter_context(tc.psum_pool(name="turned", bufs=2))
+        turned_pool = stack.enter_context(tc.psum_pool(name="turned", bufs=1))
         sums_pool = stack.enter_context(tc.psum_pool(name="sums", bufs=1))
-        acc_pool = stack.enter_context(tc.psum_pool(name="acc", bufs=2))
-        features_pool = stack.enter_context(tc.psum_pool(name="features", bufs=1))
-        rows_pool = stack.enter_context(tc.psum_pool(name="rows", bufs=2))
+        acc_pool = stack.enter_context(tc.psum_pool(name="acc", bufs=PAIR))
+        features_pool = stack.enter_context(tc.psum_pool(name="features", bufs=PAIR))
+        rows_pool = stack.enter_context(tc.psum_pool(name="rows", bufs=PAIR))
 
         identity = const.tile([P, P], F32)
         make_identity(nc, identity[:])
@@ -105,10 +109,10 @@ def tile_gnnnicheencoder_pa_t_kernel(tc, h, W_l, b_l, W_r, ln_g, ln_b, out):
         )
         vector_rows_f32 = const.tile([P, P], F32)
         nc.vector.tensor_copy(out=vector_rows_f32[:], in_=vector_rows[:])
-        turned = turned_pool.tile([P, HALVES, P], F32)
-        nc.tensor.transpose(turned[:, 0, :], vector_rows_f32[:], identity[:])
+        turned = turned_pool.tile([P, PAIR, HALVES, P], F32)
+        nc.tensor.transpose(turned[:, 0, 0, :], vector_rows_f32[:], identity[:])
         per_feature = const.tile([P, 2 * CHUNKS], F32)
-        nc.vector.tensor_copy(out=per_feature[:], in_=turned[:, 0, 0 : 2 * CHUNKS])
+        nc.vector.tensor_copy(out=per_feature[:], in_=turned[:, 0, 0, 0 : 2 * CHUNKS])
         gain = per_feature[:, 0:CHUNKS]
         shift = per_feature[:, CHUNKS : 2 * CHUNKS]
 
@@ -117,14 +121,15 @@ def tile_gnnnicheencoder_pa_t_kernel(tc, h, W_l, b_l, W_r, ln_g, ln_b, out):
 
         def load_block(s):
             block = h[s * P : (s + 1) * P, :, :]
-            nodes_on_partitions = blocks.tile([P, SUMS, D], BF16, name="by_node")
-            spread = block[:, 0:OTHERS, :].rearrange("(T g) i k -> g i T k", g=GRAPHS_PER_SUM)
+            graphs_on_partitions = blocks.tile([P, NODES, D], BF16, name="by_graph")
+            nc.sync.dma_start(out=graphs_on_partitions[:, LAST, :], in_=block[:, LAST, :])
+            nodes_on_partitions = blocks.tile([P, SUMS, D], BF16, name="by_node", bufs=2)
+            spread = block[:, 0:LAST, :].rearrange("(T g) i k -> g i T k", g=GRAPHS_PER_SUM)
             for g in range(GRAPHS_PER_SUM):
                 nc.sync.dma_start(
                     out=nodes_on_partitions[g * OTHERS : (g + 1) * OTHERS, :, :], in_=spread[g]
                 )
-            graphs_on_partitions = blocks.tile([P, NODES, D], BF16, name="by_graph")
-            nc.sync.dma_start(out=graphs_on_partitions[:], in_=block)
+            nc.sync.dma_start(out=graphs_on_partitions[:, 0:LAST, :], in_=block[:, 0:LAST, :])
             by_node.append(nodes_on_partitions)
             by_graph.append(graphs_on_partitions)
 
@@ -132,7 +137,8 @@ def tile_gnnnicheencoder_pa_t_kernel(tc, h, W_l, b_l, W_r, ln_g, ln_b, out):
         load_block(1)
 
         tiles = [(s, i) for s in range(BLOCKS) for i in [LAST] + list(range(LAST))]
-        count = len(tiles)
+        count = len(tiles) // PAIR
+        pair_of_last = [s * NODES // PAIR for s in range(BLOCKS)]
         sums_of = {}
         mean_of = {}
         kept = {}
@@ -150,162 +156,172 @@ def tile_gnnnicheencoder_pa_t_kernel(tc, h, W_l, b_l, W_r, ln_g, ln_b, out):
                     stop=True,
                 )
 
-        def block_mean(s, n):
-            mean = means.tile([P, P, PACK], F32, name="mean")
-            nc.vector.scalar_tensor_tensor(
-                out=mean[:],
-                in0=kept[("grouped", n)][:, 0, :, :],
-                scalar=1.0 / OTHERS,
-                in1=sums_of[s][:].rearrange("p t g -> p g t"),
-                op0=ALU.mult,
-                op1=ALU.add,
-            )
-            mean_of[s] = mean
+        def turn(q):
+            turned = turned_pool.tile([P, PAIR, HALVES, P], F32)
+            for j in range(PAIR):
+                s, i = tiles[PAIR * q + j]
+                turn_words(nc, identity, by_graph[s][:, i, :], turned[:, j, :, :])
+            kept[("turned", q)] = turned
 
-        def turn(n):
-            s, i = tiles[n]
-            kept[("turned", n)] = turn_words(nc, turned_pool, identity, by_graph[s][:, i, :])
+        def group(q):
+            grouped = work.tile([P, 2, PAIR, P, PACK], BF16, name="grouped", align_bytes=64, bufs=3)
+            group_words(nc, kept[("turned", q)], grouped[:, 0, :, :, :])
+            kept[("grouped", q)] = grouped
 
-        def group(n):
-            grouped = work.tile([P, 2, P, PACK], BF16, name="grouped", align_bytes=64)
-            group_words(nc, kept[("turned", n)], grouped[:, 0, :, :])
-            kept[("grouped", n)] = grouped
+        def neighbours(q):
+            grouped = kept[("grouped", q)]
+            for j in range(PAIR):
+                s, i = tiles[PAIR * q + j]
+                if i == LAST:
+                    mean = means.tile([P, P, PACK], F32, name="mean")
+                    nc.vector.scalar_tensor_tensor(
+                        out=mean[:],
+                        in0=grouped[:, 0, j, :, :],
+                        scalar=1.0 / OTHERS,
+                        in1=sums_of[s][:].rearrange("p t g -> p g t"),
+                        op0=ALU.mult,
+                        op1=ALU.add,
+                    )
+                    mean_of[s] = mean
+                nc.vector.scalar_tensor_tensor(
+                    out=grouped[:, 1, j, :, :],
+                    in0=grouped[:, 0, j, :, :],
+                    scalar=-1.0 / OTHERS,
+                    in1=mean_of[s][:],
+                    op0=ALU.mult,
+                    op1=ALU.add,
+                )
 
-        def neighbours(n):
-            s, i = tiles[n]
-            grouped = kept[("grouped", n)]
-            nc.vector.scalar_tensor_tensor(
-                out=grouped[:, 1, :, :],
-                in0=grouped[:, 0, :, :],
-                scalar=-1.0 / OTHERS,
-                in1=mean_of[s][:],
-                op0=ALU.mult,
-                op1=ALU.add,
-            )
-
-        def quantise(n):
-            codes = work.tile([P, 2, P], U32, name="codes", align_bytes=64)
-            scales = work.tile([P, 2, P], U8, name="scales", align_bytes=64)
+        def quantise(q):
+            codes = work.tile([P, 2, PAIR, P], U32, name="codes", align_bytes=64)
+            scales = work.tile([P, 2, PAIR, P], U8, name="scales", align_bytes=64)
             nc.vector.quantize_mx(
-                out=codes[:].rearrange("p x r -> p (x r)").bitcast(FP8X4),
-                scales=scales[:].rearrange("p x r -> p (x r)"),
-                in_=kept[("grouped", n)][:].rearrange("p x r t -> p (x r t)"),
+                out=codes[:].rearrange("p x j r -> p (x j r)").bitcast(FP8X4),
+                scales=scales[:].rearrange("p x j r -> p (x j r)"),
+                in_=kept[("grouped", q)][:].rearrange("p x j r t -> p (x j r t)"),
             )
-            kept[("codes", n)] = (codes, scales)
+            kept[("codes", q)] = (codes, scales)
 
-        def multiply(n):
-            codes, scales = kept[("codes", n)]
-            acc = acc_pool.tile([P, D], F32)
-            nc.tensor.matmul_mx(
-                out=acc[:],
-                lhsT=codes[:, 0, :].bitcast(FP8X4),
-                lhsT_scale=scales[:, 0, :],
-                rhs=wr_codes[:].bitcast(FP8X4),
-                rhs_scale=wr_scales[:],
-                start=True,
-                stop=False,
-            )
-            nc.tensor.matmul_mx(
-                out=acc[:],
-                lhsT=codes[:, 1, :].bitcast(FP8X4),
-                lhsT_scale=scales[:, 1, :],
-                rhs=wl_codes[:].bitcast(FP8X4),
-                rhs_scale=wl_scales[:],
-                start=False,
-                stop=True,
-            )
-            kept[("acc", n)] = acc
+        def multiply(q):
+            codes, scales = kept[("codes", q)]
+            banks = []
+            for j in range(PAIR):
+                acc = acc_pool.tile([P, D], F32)
+                nc.tensor.matmul_mx(
+                    out=acc[:],
+                    lhsT=codes[:, 0, j, :].bitcast(FP8X4),
+                    lhsT_scale=scales[:, 0, j, :],
+                    rhs=wr_codes[:].bitcast(FP8X4),
+                    rhs_scale=wr_scales[:],
+                    start=True,
+                    stop=False,
+                )
+                nc.tensor.matmul_mx(
+                    out=acc[:],
+                    lhsT=codes[:, 1, j, :].bitcast(FP8X4),
+                    lhsT_scale=scales[:, 1, j, :],
+                    rhs=wl_codes[:].bitcast(FP8X4),
+                    rhs_scale=wl_scales[:],
+                    start=False,
+                    stop=True,
+                )
+                banks.append(acc)
+            kept[("acc", q)] = banks
 
-        def add_bias(n):
-            c = work.tile([P, D], F32, name="c")
-            row_sum = stats.tile([P, 1], F32, name="row_sum")
-            nc.vector.scalar_tensor_tensor(
-                out=c[:],
-                in0=kept[("acc", n)][:],
-                scalar=1.0,
-                in1=bias_rows[:],
-                op0=ALU.mult,
-                op1=ALU.add,
-                accum_out=row_sum[:],
-            )
-            kept[("c", n)] = c
-            kept[("row_sum", n)] = row_sum
+        def add_bias(q):
+            c = work.tile([P, PAIR, D], F32, name="c", bufs=3)
+            row_sum = stats.tile([P, PAIR], F32, name="row_sum")
+            for j in range(PAIR):
+                nc.vector.scalar_tensor_tensor(
+                    out=c[:, j, :],
+                    in0=kept[("acc", q)][j][:],
+                    scalar=1.0,
+                    in1=bias_rows[:],
+                    op0=ALU.mult,
+                    op1=ALU.add,
+                    accum_out=row_sum[:, j : j + 1],
+                )
+            kept[("c", q)] = c
+            kept[("row_sum", q)] = row_sum
 
-        def negate_mean(n):
-            minus_mean = stats.tile([P, 1], F32, name="minus_mean")
-            nc.scalar.mul(out=minus_mean[:], in_=kept[("row_sum", n)][:], mul=-1.0 / D)
-            kept[("minus_mean", n)] = minus_mean
+        def negate_mean(q):
+            minus_mean = stats.tile([P, PAIR], F32, name="minus_mean")
+            nc.scalar.mul(out=minus_mean[:], in_=kept[("row_sum", q)][:], mul=-1.0 / D)
+            kept[("minus_mean", q)] = minus_mean
 
-        def sum_squares(n):
-            squares = work.tile([P, D], BF16, name="squares")
-            square_sum = stats.tile([P, 1], F32, name="square_sum")
-            nc.scalar.activation(
-                out=squares[:],
-                in_=kept[("c", n)][:],
-                func=ACT.Square,
-                bias=kept[("minus_mean", n)][:],
-                scale=1.0,
-                accum_out=square_sum[:],
-            )
-            kept[("square_sum", n)] = square_sum
+        def sum_squares(q):
+            square_sum = stats.tile([P, PAIR], F32, name="square_sum")
+            for j in range(PAIR):
+                squares = work.tile([P, D], BF16, name="squares")
+                nc.scalar.activation(
+                    out=squares[:],
+                    in_=kept[("c", q)][:, j, :],
+                    func=ACT.Square,
+                    bias=kept[("minus_mean", q)][:, j : j + 1],
+                    scale=1.0,
+                    accum_out=square_sum[:, j : j + 1],
+                )
+            kept[("square_sum", q)] = square_sum
 
-        def invert_deviation(n):
-            inverse = stats.tile([P, 1], F32, name="inverse")
+        def invert_deviation(q):
+            inverse = stats.tile([P, PAIR], F32, name="inverse")
             nc.scalar.activation(
                 out=inverse[:],
-                in_=kept[("square_sum", n)][:],
+                in_=kept[("square_sum", q)][:],
                 func=ACT.Abs_reciprocal_sqrt,
                 bias=eps[:],
                 scale=1.0 / D,
             )
-            kept[("inverse", n)] = inverse
+            kept[("inverse", q)] = inverse
 
-        def fold_mean(n):
-            offset = stats.tile([P, 1], F32, name="offset")
-            nc.scalar.activation(
-                out=offset[:],
-                in_=kept[("minus_mean", n)][:],
-                func=ACT.Copy,
-                scale=kept[("inverse", n)][:],
+        def fold_mean(q):
+            offset = stats.tile([P, PAIR], F32, name="offset")
+            nc.vector.tensor_mul(
+                out=offset[:], in0=kept[("minus_mean", q)][:], in1=kept[("inverse", q)][:]
             )
-            kept[("offset", n)] = offset
+            kept[("offset", q)] = offset
 
-        def normalise(n):
-            normal = work.tile([P, D], F32, name="normal")
-            nc.scalar.activation(
-                out=normal[:],
-                in_=kept[("c", n)][:],
-                func=ACT.Identity,
-                bias=kept[("offset", n)][:],
-                scale=kept[("inverse", n)][:],
-            )
-            kept[("normal", n)] = normal
-
-        def to_features(n):
-            normal = kept[("normal", n)]
-            normal_turned = features_pool.tile([P, CHUNKS, P], F32)
-            for f in range(CHUNKS):
-                nc.tensor.transpose(
-                    normal_turned[:, f, :], normal[:, f * P : (f + 1) * P], identity[:]
+        def normalise(q):
+            normal = work.tile([P, PAIR, D], F32, name="normal")
+            for j in range(PAIR):
+                nc.scalar.activation(
+                    out=normal[:, j, :],
+                    in_=kept[("c", q)][:, j, :],
+                    func=ACT.Identity,
+                    bias=kept[("offset", q)][:, j : j + 1],
+                    scale=kept[("inverse", q)][:, j : j + 1],
                 )
-            kept[("normal_turned", n)] = normal_turned
+            kept[("normal", q)] = normal
 
-        def gain_and_shift(n):
-            normal_turned = kept[("normal_turned", n)]
-            y_turned = work.tile([P, CHUNKS, P], F32, name="y_turned")
+        def to_features(q):
+            normal = kept[("normal", q)]
+            banks = []
+            for half in range(CHUNKS // 2):
+                normal_turned = features_pool.tile([P, 2, PAIR, P], F32)
+                for x in range(2):
+                    f = 2 * half + x
+                    for j in range(PAIR):
+                        nc.tensor.transpose(
+                            normal_turned[:, x, j, :], normal[:, j, f * P : (f + 1) * P], identity[:]
+                        )
+                banks.append(normal_turned)
+            kept[("normal_turned", q)] = banks
+
+        def gain_and_shift(q):
+            y_turned = work.tile([P, CHUNKS, PAIR, P], F32, name="y_turned")
             for f in range(CHUNKS):
                 nc.scalar.activation(
-                    out=y_turned[:, f, :],
-                    in_=normal_turned[:, f, :],
+                    out=y_turned[:, f, :, :],
+                    in_=kept[("normal_turned", q)][f // 2][:, f % 2, :, :],
                     func=ACT.Identity,
                     bias=shift[:, f : f + 1],
                     scale=gain[:, f : f + 1],
                 )
-            kept[("y_turned", n)] = y_turned
+            kept[("y_turned", q)] = y_turned
 
-        def leaky_relu(n):
-            y_turned = kept[("y_turned", n)]
-            a_turned = work.tile([P, CHUNKS, P], F32, name="a_turned")
+        def leaky_relu(q):
+            y_turned = kept[("y_turned", q)]
+            a_turned = work.tile([P, CHUNKS, PAIR, P], F32, name="a_turned")
             nc.vector.scalar_tensor_tensor(
                 out=a_turned[:],
                 in0=y_turned[:],
@@ -314,48 +330,58 @@ def tile_gnnnicheencoder_pa_t_kernel(tc, h, W_l, b_l, W_r, ln_g, ln_b, out):
                 op0=ALU.mult,
                 op1=ALU.max,
             )
-            kept[("a_turned", n)] = a_turned
+            kept[("a_turned", q)] = a_turned
 
-        def to_rows(n):
-            a_turned = kept[("a_turned", n)]
-            a_rows = rows_pool.tile([P, D], F32)
-            for f in range(CHUNKS):
-                nc.tensor.transpose(a_rows[:, f * P : (f + 1) * P], a_turned[:, f, :], identity[:])
-            kept[("a_rows", n)] = a_rows
+        def to_rows(q):
+            a_turned = kept[("a_turned", q)]
+            banks = []
+            for j in range(PAIR):
+                a_rows = rows_pool.tile([P, D], F32)
+                for f in range(CHUNKS):
+                    nc.tensor.transpose(
+                        a_rows[:, f * P : (f + 1) * P], a_turned[:, f, j, :], identity[:]
+                    )
+                banks.append(a_rows)
+            kept[("a_rows", q)] = banks
 
-        def add_residual(n):
-            s, i = tiles[n]
-            result = work.tile([P, D], F32, name="result")
-            nc.vector.tensor_add(out=result[:], in0=kept[("a_rows", n)][:], in1=by_graph[s][:, i, :])
-            nc.sync.dma_start(out=out[s * P : (s + 1) * P, i, :], in_=result[:])
+        def add_residual(q):
+            for j in range(PAIR):
+                s, i = tiles[PAIR * q + j]
+                result = work.tile([P, D], F32, name="result", bufs=4)
+                nc.vector.tensor_add(
+                    out=result[:], in0=kept[("a_rows", q)][j][:], in1=by_graph[s][:, i, :]
+                )
+                nc.sync.dma_start(out=out[s * P : (s + 1) * P, i, :], in_=result[:])
 
-        def run(stage_of_tile, n):
-            if 0 <= n < count:
-                stage_of_tile(n)
+        def run(stage_of_pair, q):
+            if 0 <= q < count:
+                stage_of_pair(q)
 
         for T in range(SUMS):
             sum_nodes(0, T)
 
         for k in range(count + DEPTH):
-            if k % NODES == 0 and k // NODES + 2 < BLOCKS:
-                load_block(k // NODES + 2)
-            if 0 <= k - 1 < count and tiles[k - 1][1] == LAST:
-                block_mean(tiles[k - 1][0], k - 1)
+            for s in range(2, BLOCKS):
+                if k == pair_of_last[s - 2]:
+                    load_block(s)
             run(multiply, k - 3)
-            run(to_features, k - 7)
+            run(to_features, k - 6)
             run(to_rows, k - DEPTH)
             run(turn, k)
-            if k < count and k % NODES > 0 and k // NODES + 1 < BLOCKS:
-                sum_nodes(k // NODES + 1, k % NODES - 1)
+            for s in range(1, BLOCKS):
+                first = pair_of_last[s - 1] + 2
+                if first <= k < first + SUMS // SUMS_PER_STEP:
+                    for T in range(SUMS_PER_STEP * (k - first), SUMS_PER_STEP * (k - first + 1)):
+                        sum_nodes(s, T)
+            run(fold_mean, k - 5)
+            run(group, k - 1)
             run(negate_mean, k - 4)
-            run(normalise, k - 6)
+            run(normalise, k - 5)
             run(sum_squares, k - 4)
-            run(gain_and_shift, k - 7)
+            run(gain_and_shift, k - 6)
             run(invert_deviation, k - 4)
-            run(group, k)
-            run(fold_mean, k - 4)
-            run(neighbours, k - 1)
+            run(leaky_relu, k - 7)
             run(quantise, k - 2)
-            run(leaky_relu, k - 8)
+            run(neighbours, k - 1)
             run(add_bias, k - 3)
             run(add_residual, k - DEPTH)

@@ -29,6 +29,7 @@ LN_EPS = 1e-5
 LEAKY_SLOPE = 0.01
 PAIR = 2
 SUMS_PER_STEP = 4
+LOADS_PER_STEP = 2
 DEPTH = 8
 
 FLOPS = 2 * 2 * GRAPHS * NODES * D * D
@@ -83,7 +84,7 @@ def tile_gnnnicheencoder_pa_t_kernel(tc, h, W_l, b_l, W_r, ln_g, ln_b, out):
         graph_of_partition = const.tile([P, GRAPHS_PER_SUM], F32)
         nc.vector.tensor_reduce(
             out=graph_of_partition[:],
-            in_=identity[:].rearrange("p (g i) -> p g i", i=OTHERS),
+            in_=identity[:].rearrange("p (i g) -> p g i", g=GRAPHS_PER_SUM),
             axis=AXIS.X,
             op=ALU.add,
         )
@@ -116,25 +117,26 @@ def tile_gnnnicheencoder_pa_t_kernel(tc, h, W_l, b_l, W_r, ln_g, ln_b, out):
         gain = per_feature[:, 0:CHUNKS]
         shift = per_feature[:, CHUNKS : 2 * CHUNKS]
 
-        by_graph = []
-        by_node = []
+        by_graph = {}
+        by_node = {}
 
-        def load_block(s):
+        def load_graphs(s):
             block = h[s * P : (s + 1) * P, :, :]
-            graphs_on_partitions = blocks.tile([P, NODES, D], BF16, name="by_graph")
-            nc.sync.dma_start(out=graphs_on_partitions[:, LAST, :], in_=block[:, LAST, :])
-            nodes_on_partitions = blocks.tile([P, SUMS, D], BF16, name="by_node", bufs=2)
-            spread = block[:, 0:LAST, :].rearrange("(T g) i k -> g i T k", g=GRAPHS_PER_SUM)
-            for g in range(GRAPHS_PER_SUM):
-                nc.sync.dma_start(
-                    out=nodes_on_partitions[g * OTHERS : (g + 1) * OTHERS, :, :], in_=spread[g]
-                )
-            nc.sync.dma_start(out=graphs_on_partitions[:, 0:LAST, :], in_=block[:, 0:LAST, :])
-            by_node.append(nodes_on_partitions)
-            by_graph.append(graphs_on_partitions)
+            by_graph[s] = blocks.tile([P, NODES, D], BF16, name="by_graph")
+            nc.sync.dma_start(out=by_graph[s][:, LAST, :], in_=block[:, LAST, :])
+            nc.sync.dma_start(out=by_graph[s][:, 0:LAST, :], in_=block[:, 0:LAST, :])
 
-        load_block(0)
-        load_block(1)
+        def load_nodes(s, g):
+            if g == 0:
+                by_node[s] = blocks.tile([P, SUMS, D], BF16, name="by_node", bufs=2)
+            spread = h[s * P : (s + 1) * P, 0:LAST, :].rearrange(
+                "(T g) i k -> g i T k", g=GRAPHS_PER_SUM
+            )
+            nc.sync.dma_start(out=by_node[s][g:P:GRAPHS_PER_SUM, :, :], in_=spread[g])
+
+        for g in range(GRAPHS_PER_SUM):
+            load_nodes(0, g)
+        load_graphs(0)
 
         tiles = [(s, i) for s in range(BLOCKS) for i in [LAST] + list(range(LAST))]
         count = len(tiles) // PAIR
@@ -361,15 +363,19 @@ def tile_gnnnicheencoder_pa_t_kernel(tc, h, W_l, b_l, W_r, ln_g, ln_b, out):
             sum_nodes(0, T)
 
         for k in range(count + DEPTH):
-            for s in range(2, BLOCKS):
-                if k == pair_of_last[s - 2]:
-                    load_block(s)
+            for s in range(1, BLOCKS):
+                since = k - pair_of_last[s - 1]
+                if 0 <= since < GRAPHS_PER_SUM // LOADS_PER_STEP:
+                    for g in range(LOADS_PER_STEP * since, LOADS_PER_STEP * (since + 1)):
+                        load_nodes(s, g)
+                if since == GRAPHS_PER_SUM // LOADS_PER_STEP:
+                    load_graphs(s)
             run(multiply, k - 3)
             run(to_features, k - 6)
             run(to_rows, k - DEPTH)
             run(turn, k)
             for s in range(1, BLOCKS):
-                first = pair_of_last[s - 1] + 2
+                first = pair_of_last[s] + 1 - SUMS // SUMS_PER_STEP
                 if first <= k < first + SUMS // SUMS_PER_STEP:
                     for T in range(SUMS_PER_STEP * (k - first), SUMS_PER_STEP * (k - first + 1)):
                         sum_nodes(s, T)

@@ -90,6 +90,8 @@ def tile_gnnnicheencoder_pa_t_kernel(tc, h, W_l, b_l, W_r, ln_g, ln_b, out):
         )
         node_sum = const.tile([P, GRAPHS_PER_SUM], BF16)
         nc.vector.tensor_scalar_mul(out=node_sum[:], in0=graph_of_partition[:], scalar1=1.0 / OTHERS)
+        sixteenth = const.tile([P, P], BF16)
+        nc.vector.tensor_scalar_mul(out=sixteenth[:], in0=identity[:], scalar1=1.0 / OTHERS)
         eps = const.tile([P, 1], F32)
         nc.vector.memset(eps[:], LN_EPS)
         vector_rows = const.tile([P, P], BF16)
@@ -101,21 +103,6 @@ def tile_gnnnicheencoder_pa_t_kernel(tc, h, W_l, b_l, W_r, ln_g, ln_b, out):
         wl_scales = const.tile([P, D], U8, align_bytes=64)
         quantise_weight(nc, stage, turned_pool, identity, W_r, wr_codes, wr_scales)
         quantise_weight(nc, stage, turned_pool, identity, W_l, wl_codes, wl_scales)
-
-        bias_rows = const.tile([P, D], BF16)
-        nc.sync.dma_start(out=bias_rows[:], in_=b_l.partition_broadcast(P))
-        nc.sync.dma_start(out=vector_rows[0:CHUNKS, :], in_=ln_g.rearrange("(f p) -> f p", p=P))
-        nc.sync.dma_start(
-            out=vector_rows[CHUNKS : 2 * CHUNKS, :], in_=ln_b.rearrange("(f p) -> f p", p=P)
-        )
-        vector_rows_f32 = const.tile([P, P], F32)
-        nc.vector.tensor_copy(out=vector_rows_f32[:], in_=vector_rows[:])
-        turned = turned_pool.tile([P, PAIR, HALVES, P], F32)
-        nc.tensor.transpose(turned[:, 0, 0, :], vector_rows_f32[:], identity[:])
-        per_feature = const.tile([P, 2 * CHUNKS], F32)
-        nc.vector.tensor_copy(out=per_feature[:], in_=turned[:, 0, 0, 0 : 2 * CHUNKS])
-        gain = per_feature[:, 0:CHUNKS]
-        shift = per_feature[:, CHUNKS : 2 * CHUNKS]
 
         by_graph = {}
         by_node = {}
@@ -134,9 +121,13 @@ def tile_gnnnicheencoder_pa_t_kernel(tc, h, W_l, b_l, W_r, ln_g, ln_b, out):
             )
             nc.sync.dma_start(out=by_node[s][g:P:GRAPHS_PER_SUM, :, :], in_=spread[g])
 
-        for g in range(GRAPHS_PER_SUM):
-            load_nodes(0, g)
         load_graphs(0)
+        bias_rows = const.tile([P, D], BF16)
+        nc.sync.dma_start(out=bias_rows[:], in_=b_l.partition_broadcast(P))
+        nc.sync.dma_start(out=vector_rows[0:CHUNKS, :], in_=ln_g.rearrange("(f p) -> f p", p=P))
+        nc.sync.dma_start(
+            out=vector_rows[CHUNKS : 2 * CHUNKS, :], in_=ln_b.rearrange("(f p) -> f p", p=P)
+        )
 
         tiles = [(s, i) for s in range(BLOCKS) for i in [LAST] + list(range(LAST))]
         count = len(tiles) // PAIR
@@ -157,6 +148,19 @@ def tile_gnnnicheencoder_pa_t_kernel(tc, h, W_l, b_l, W_r, ln_g, ln_b, out):
                     start=True,
                     stop=True,
                 )
+
+        def sum_nodes_of_first_block():
+            sums_of[0] = sums_pool.tile([P, PACK, P], F32, name="sums")
+            for t in range(PACK):
+                for i in range(LAST):
+                    columns = by_graph[0][:, i, :].rearrange("p (u q e) -> p u e q", u=HALVES, e=2)
+                    nc.tensor.matmul(
+                        out=sums_of[0][:, t, :],
+                        lhsT=columns[:, t // 2, t % 2, :],
+                        rhs=sixteenth[:],
+                        start=(i == 0),
+                        stop=(i == LAST - 1),
+                    )
 
         def turn(q):
             turned = turned_pool.tile([P, PAIR, HALVES, P], F32)
@@ -359,8 +363,16 @@ def tile_gnnnicheencoder_pa_t_kernel(tc, h, W_l, b_l, W_r, ln_g, ln_b, out):
             if 0 <= q < count:
                 stage_of_pair(q)
 
-        for T in range(SUMS):
-            sum_nodes(0, T)
+        sum_nodes_of_first_block()
+
+        vector_rows_f32 = const.tile([P, P], F32)
+        nc.vector.tensor_copy(out=vector_rows_f32[:], in_=vector_rows[:])
+        turned = turned_pool.tile([P, PAIR, HALVES, P], F32)
+        nc.tensor.transpose(turned[:, 0, 0, :], vector_rows_f32[:], identity[:])
+        per_feature = const.tile([P, 2 * CHUNKS], F32)
+        nc.vector.tensor_copy(out=per_feature[:], in_=turned[:, 0, 0, 0 : 2 * CHUNKS])
+        gain = per_feature[:, 0:CHUNKS]
+        shift = per_feature[:, CHUNKS : 2 * CHUNKS]
 
         for k in range(count + DEPTH):
             for s in range(1, BLOCKS):

@@ -30,7 +30,7 @@ LEAKY_SLOPE = 0.01
 PAIR = 2
 SUMS_PER_STEP = 4
 LOADS_PER_STEP = 2
-DEPTH = 8
+DEPTH = 7
 
 FLOPS = 2 * 2 * GRAPHS * NODES * D * D
 
@@ -280,22 +280,16 @@ def tile_gnnnicheencoder_pa_t_kernel(tc, h, W_l, b_l, W_r, ln_g, ln_b, out):
             )
             kept[("inverse", q)] = inverse
 
-        def fold_mean(q):
-            offset = stats.tile([P, PAIR], F32, name="offset")
-            nc.vector.tensor_mul(
-                out=offset[:], in0=kept[("minus_mean", q)][:], in1=kept[("inverse", q)][:]
-            )
-            kept[("offset", q)] = offset
-
         def normalise(q):
             normal = work.tile([P, PAIR, D], F32, name="normal")
             for j in range(PAIR):
-                nc.scalar.activation(
+                nc.vector.tensor_scalar(
                     out=normal[:, j, :],
-                    in_=kept[("c", q)][:, j, :],
-                    func=ACT.Identity,
-                    bias=kept[("offset", q)][:, j : j + 1],
-                    scale=kept[("inverse", q)][:, j : j + 1],
+                    in0=kept[("c", q)][:, j, :],
+                    scalar1=kept[("minus_mean", q)][:, j : j + 1],
+                    scalar2=kept[("inverse", q)][:, j : j + 1],
+                    op0=ALU.add,
+                    op1=ALU.mult,
                 )
             kept[("normal", q)] = normal
 
@@ -313,39 +307,48 @@ def tile_gnnnicheencoder_pa_t_kernel(tc, h, W_l, b_l, W_r, ln_g, ln_b, out):
                 banks.append(normal_turned)
             kept[("normal_turned", q)] = banks
 
-        def gain_and_shift(q):
-            y_turned = work.tile([P, CHUNKS, PAIR, P], F32, name="y_turned")
+        def two_terms(q):
+            bent = work.tile([P, CHUNKS, PAIR, P], F32, name="bent")
+            straight = work.tile([P, CHUNKS, PAIR, P], F32, name="straight")
             for f in range(CHUNKS):
+                normal_turned = kept[("normal_turned", q)][f // 2][:, f % 2, :, :]
                 nc.scalar.activation(
-                    out=y_turned[:, f, :, :],
-                    in_=kept[("normal_turned", q)][f // 2][:, f % 2, :, :],
-                    func=ACT.Identity,
-                    bias=shift[:, f : f + 1],
-                    scale=gain[:, f : f + 1],
+                    out=bent[:, f, :, :],
+                    in_=normal_turned,
+                    func=ACT.Relu,
+                    bias=relu_term[:, CHUNKS + f : CHUNKS + f + 1],
+                    scale=relu_term[:, f : f + 1],
                 )
-            kept[("y_turned", q)] = y_turned
-
-        def leaky_relu(q):
-            y_turned = kept[("y_turned", q)]
-            a_turned = work.tile([P, CHUNKS, PAIR, P], F32, name="a_turned")
-            nc.vector.scalar_tensor_tensor(
-                out=a_turned[:],
-                in0=y_turned[:],
-                scalar=LEAKY_SLOPE,
-                in1=y_turned[:],
-                op0=ALU.mult,
-                op1=ALU.max,
-            )
-            kept[("a_turned", q)] = a_turned
+                nc.scalar.activation(
+                    out=straight[:, f, :, :],
+                    in_=normal_turned,
+                    func=ACT.Identity,
+                    bias=line_term[:, CHUNKS + f : CHUNKS + f + 1],
+                    scale=line_term[:, f : f + 1],
+                )
+            kept[("terms", q)] = (bent, straight)
 
         def to_rows(q):
-            a_turned = kept[("a_turned", q)]
+            bent, straight = kept[("terms", q)]
             banks = []
             for j in range(PAIR):
                 a_rows = rows_pool.tile([P, D], F32)
                 for f in range(CHUNKS):
-                    nc.tensor.transpose(
-                        a_rows[:, f * P : (f + 1) * P], a_turned[:, f, j, :], identity[:]
+                    nc.tensor.matmul(
+                        out=a_rows[:, f * P : (f + 1) * P],
+                        lhsT=bent[:, f, j, :],
+                        rhs=identity[:],
+                        is_transpose=True,
+                        start=True,
+                        stop=False,
+                    )
+                    nc.tensor.matmul(
+                        out=a_rows[:, f * P : (f + 1) * P],
+                        lhsT=straight[:, f, j, :],
+                        rhs=identity[:],
+                        is_transpose=True,
+                        start=False,
+                        stop=True,
                     )
                 banks.append(a_rows)
             kept[("a_rows", q)] = banks
@@ -371,8 +374,10 @@ def tile_gnnnicheencoder_pa_t_kernel(tc, h, W_l, b_l, W_r, ln_g, ln_b, out):
         nc.tensor.transpose(turned[:, 0, 0, :], vector_rows_f32[:], identity[:])
         per_feature = const.tile([P, 2 * CHUNKS], F32)
         nc.vector.tensor_copy(out=per_feature[:], in_=turned[:, 0, 0, 0 : 2 * CHUNKS])
-        gain = per_feature[:, 0:CHUNKS]
-        shift = per_feature[:, CHUNKS : 2 * CHUNKS]
+        relu_term = const.tile([P, 2 * CHUNKS], F32)
+        nc.vector.tensor_scalar_mul(out=relu_term[:], in0=per_feature[:], scalar1=1.0 - LEAKY_SLOPE)
+        line_term = const.tile([P, 2 * CHUNKS], F32)
+        nc.vector.tensor_scalar_mul(out=line_term[:], in0=per_feature[:], scalar1=LEAKY_SLOPE)
 
         for k in range(count + DEPTH):
             for s in range(1, BLOCKS):
@@ -391,14 +396,12 @@ def tile_gnnnicheencoder_pa_t_kernel(tc, h, W_l, b_l, W_r, ln_g, ln_b, out):
                 if first <= k < first + SUMS // SUMS_PER_STEP:
                     for T in range(SUMS_PER_STEP * (k - first), SUMS_PER_STEP * (k - first + 1)):
                         sum_nodes(s, T)
-            run(fold_mean, k - 5)
-            run(group, k - 1)
             run(negate_mean, k - 4)
-            run(normalise, k - 5)
+            run(group, k - 1)
             run(sum_squares, k - 4)
-            run(gain_and_shift, k - 6)
+            run(two_terms, k - 6)
             run(invert_deviation, k - 4)
-            run(leaky_relu, k - 7)
+            run(normalise, k - 5)
             run(quantise, k - 2)
             run(neighbours, k - 1)
             run(add_bias, k - 3)

@@ -30,7 +30,7 @@ LEAKY_SLOPE = 0.01
 PAIR = 2
 SUMS_PER_STEP = 4
 LOADS_PER_STEP = 2
-DEPTH = 7
+DEPTH = 9
 
 FLOPS = 2 * 2 * GRAPHS * NODES * D * D
 
@@ -283,7 +283,7 @@ def tile_gnnnicheencoder_pa_t_kernel(tc, h, W_l, b_l, W_r, ln_g, ln_b, out):
         def normalise(q):
             normal = work.tile([P, PAIR, D], F32, name="normal")
             for j in range(PAIR):
-                nc.vector.tensor_scalar(
+                nc.gpsimd.tensor_scalar(
                     out=normal[:, j, :],
                     in0=kept[("c", q)][:, j, :],
                     scalar1=kept[("minus_mean", q)][:, j : j + 1],
@@ -387,22 +387,22 @@ def tile_gnnnicheencoder_pa_t_kernel(tc, h, W_l, b_l, W_r, ln_g, ln_b, out):
                         load_nodes(s, g)
                 if since == GRAPHS_PER_SUM // LOADS_PER_STEP:
                     load_graphs(s)
-            run(multiply, k - 3)
-            run(to_features, k - 6)
-            run(to_rows, k - DEPTH)
+            run(add_residual, k - 9)
+            run(add_bias, k - 4)
+            run(normalise, k - 6)
+            run(negate_mean, k - 5)
+            run(group, k - 1)
+            run(to_features, k - 7)
+            run(to_rows, k - 8)
             run(turn, k)
             for s in range(1, BLOCKS):
                 first = pair_of_last[s] + 1 - SUMS // SUMS_PER_STEP
                 if first <= k < first + SUMS // SUMS_PER_STEP:
                     for T in range(SUMS_PER_STEP * (k - first), SUMS_PER_STEP * (k - first + 1)):
                         sum_nodes(s, T)
-            run(negate_mean, k - 4)
-            run(group, k - 1)
-            run(sum_squares, k - 4)
-            run(two_terms, k - 6)
-            run(invert_deviation, k - 4)
-            run(normalise, k - 5)
+            run(multiply, k - 3)
+            run(sum_squares, k - 5)
+            run(two_terms, k - 7)
+            run(invert_deviation, k - 5)
             run(quantise, k - 2)
             run(neighbours, k - 1)
-            run(add_bias, k - 3)
-            run(add_residual, k - DEPTH)

@@ -15,11 +15,13 @@ AXIS = mybir.AxisListType
 
 P = 128
 PACK = 4
+WORD = 2
 HALVES = 2
 GRAPHS = 512
 NODES = 17
 D = 512
 CHUNKS = D // P
+CHUNKS_PER_BANK = 2
 BLOCKS = GRAPHS // P
 OTHERS = NODES - 1
 LAST = NODES - 1
@@ -28,9 +30,21 @@ SUMS = P // GRAPHS_PER_SUM
 LN_EPS = 1e-5
 LEAKY_SLOPE = 0.01
 PAIR = 2
+OPERANDS = 2
 SUMS_PER_STEP = 4
 LOADS_PER_STEP = 2
-DEPTH = 9
+NODES_PER_LOAD = 4
+
+AT_TURN = 0
+AT_GROUP = 1
+AT_QUANTISE = 2
+AT_MULTIPLY = 3
+AT_BIAS = 4
+AT_STATISTICS = 5
+AT_NORMALISE = 6
+AT_FEATURES = 7
+AT_ROWS = 8
+AT_RESIDUAL = 9
 
 FLOPS = 2 * 2 * GRAPHS * NODES * D * D
 
@@ -45,10 +59,10 @@ def group_words(nc, turned, grouped):
     nc.scalar.copy(out=grouped.bitcast(F32), in_=turned[:].rearrange("p j u r -> p j r u"))
 
 
-def quantise_weight(nc, stage, turned_pool, identity, weight, codes, scales):
-    rows = stage.tile([P, CHUNKS, D], BF16, name="weight_rows")
+def quantise_weight(nc, staging, turned_pool, identity, weight, codes, scales):
+    rows = staging.tile([P, CHUNKS, D], BF16, name="weight_rows")
     nc.sync.dma_start(out=rows[:], in_=weight.rearrange("(a p) k -> p a k", p=P))
-    grouped = stage.tile([P, D, PACK], BF16, name="weight_grouped", align_bytes=64)
+    grouped = staging.tile([P, D, PACK], BF16, name="weight_grouped", align_bytes=64)
     for a in range(0, CHUNKS, PAIR):
         turned = turned_pool.tile([P, PAIR, HALVES, P], F32)
         for j in range(PAIR):
@@ -68,7 +82,7 @@ def tile_gnnnicheencoder_pa_t_kernel(tc, h, W_l, b_l, W_r, ln_g, ln_b, out):
     with ExitStack() as stack:
         stack.enter_context(tc.manual_schedule())
         const = stack.enter_context(tc.tile_pool(name="const", bufs=1))
-        stage = stack.enter_context(tc.tile_pool(name="stage", bufs=2))
+        staging = stack.enter_context(tc.tile_pool(name="stage", bufs=2))
         blocks = stack.enter_context(tc.tile_pool(name="blocks", bufs=BLOCKS))
         means = stack.enter_context(tc.tile_pool(name="means", bufs=2))
         work = stack.enter_context(tc.tile_pool(name="work", bufs=2))
@@ -94,6 +108,8 @@ def tile_gnnnicheencoder_pa_t_kernel(tc, h, W_l, b_l, W_r, ln_g, ln_b, out):
         nc.vector.tensor_scalar_mul(out=sixteenth[:], in0=identity[:], scalar1=1.0 / OTHERS)
         eps = const.tile([P, 1], F32)
         nc.vector.memset(eps[:], LN_EPS)
+        first_function = const.tile([P, 1], F32)
+        nc.scalar.activation(out=first_function[:], in_=eps[:], func=ACT.Abs_reciprocal_sqrt)
         vector_rows = const.tile([P, P], BF16)
         nc.vector.memset(vector_rows[:].bitcast(I32), 0)
 
@@ -101,8 +117,8 @@ def tile_gnnnicheencoder_pa_t_kernel(tc, h, W_l, b_l, W_r, ln_g, ln_b, out):
         wr_scales = const.tile([P, D], U8, align_bytes=64)
         wl_codes = const.tile([P, D], U32, align_bytes=64)
         wl_scales = const.tile([P, D], U8, align_bytes=64)
-        quantise_weight(nc, stage, turned_pool, identity, W_r, wr_codes, wr_scales)
-        quantise_weight(nc, stage, turned_pool, identity, W_l, wl_codes, wl_scales)
+        quantise_weight(nc, staging, turned_pool, identity, W_r, wr_codes, wr_scales)
+        quantise_weight(nc, staging, turned_pool, identity, W_l, wl_codes, wl_scales)
 
         by_graph = {}
         by_node = {}
@@ -111,7 +127,10 @@ def tile_gnnnicheencoder_pa_t_kernel(tc, h, W_l, b_l, W_r, ln_g, ln_b, out):
             block = h[s * P : (s + 1) * P, :, :]
             by_graph[s] = blocks.tile([P, NODES, D], BF16, name="by_graph")
             nc.sync.dma_start(out=by_graph[s][:, LAST, :], in_=block[:, LAST, :])
-            nc.sync.dma_start(out=by_graph[s][:, 0:LAST, :], in_=block[:, 0:LAST, :])
+            for i in range(0, LAST, NODES_PER_LOAD):
+                nc.sync.dma_start(
+                    out=by_graph[s][:, i : i + NODES_PER_LOAD, :], in_=block[:, i : i + NODES_PER_LOAD, :]
+                )
 
         def load_nodes(s, g):
             if g == 0:
@@ -131,7 +150,7 @@ def tile_gnnnicheencoder_pa_t_kernel(tc, h, W_l, b_l, W_r, ln_g, ln_b, out):
 
         tiles = [(s, i) for s in range(BLOCKS) for i in [LAST] + list(range(LAST))]
         count = len(tiles) // PAIR
-        pair_of_last = [s * NODES // PAIR for s in range(BLOCKS)]
+        first_pair = [s * NODES // PAIR for s in range(BLOCKS)]
         sums_of = {}
         mean_of = {}
         kept = {}
@@ -139,28 +158,34 @@ def tile_gnnnicheencoder_pa_t_kernel(tc, h, W_l, b_l, W_r, ln_g, ln_b, out):
         def sum_nodes(s, T):
             if T == 0:
                 sums_of[s] = sums_pool.tile([P, PACK, P], F32, name="sums")
-            columns = by_node[s][:, T, :].rearrange("p (u q e) -> p u e q", u=HALVES, e=2)
+            columns = by_node[s][:, T, :].rearrange("p (u q e) -> p u e q", u=HALVES, e=WORD)
             for t in range(PACK):
                 nc.tensor.matmul(
                     out=sums_of[s][:, t, T * GRAPHS_PER_SUM : (T + 1) * GRAPHS_PER_SUM],
-                    lhsT=columns[:, t // 2, t % 2, :],
+                    lhsT=columns[:, t // WORD, t % WORD, :],
                     rhs=node_sum[:],
                     start=True,
                     stop=True,
                 )
 
         def sum_nodes_of_first_block():
+            total = acc_pool.tile([P, D], F32, name="acc")
+            for i in range(LAST):
+                nc.tensor.matmul(
+                    out=total[:],
+                    lhsT=sixteenth[:],
+                    rhs=by_graph[0][:, i, :],
+                    start=(i == 0),
+                    stop=(i == LAST - 1),
+                )
+            total_rows = const.tile([P, D], F32)
+            nc.scalar.copy(out=total_rows[:], in_=total[:])
             sums_of[0] = sums_pool.tile([P, PACK, P], F32, name="sums")
+            columns = total_rows[:].rearrange("p (u q e) -> p u e q", u=HALVES, e=WORD)
             for t in range(PACK):
-                for i in range(LAST):
-                    columns = by_graph[0][:, i, :].rearrange("p (u q e) -> p u e q", u=HALVES, e=2)
-                    nc.tensor.matmul(
-                        out=sums_of[0][:, t, :],
-                        lhsT=columns[:, t // 2, t % 2, :],
-                        rhs=sixteenth[:],
-                        start=(i == 0),
-                        stop=(i == LAST - 1),
-                    )
+                nc.tensor.transpose(
+                    sums_of[0][:, t, :], columns[:, t // WORD, t % WORD, :], identity[:]
+                )
 
         def turn(q):
             turned = turned_pool.tile([P, PAIR, HALVES, P], F32)
@@ -170,7 +195,9 @@ def tile_gnnnicheencoder_pa_t_kernel(tc, h, W_l, b_l, W_r, ln_g, ln_b, out):
             kept[("turned", q)] = turned
 
         def group(q):
-            grouped = work.tile([P, 2, PAIR, P, PACK], BF16, name="grouped", align_bytes=64, bufs=3)
+            grouped = work.tile(
+                [P, OPERANDS, PAIR, P, PACK], BF16, name="grouped", align_bytes=64, bufs=3
+            )
             group_words(nc, kept[("turned", q)], grouped[:, 0, :, :, :])
             kept[("grouped", q)] = grouped
 
@@ -199,8 +226,8 @@ def tile_gnnnicheencoder_pa_t_kernel(tc, h, W_l, b_l, W_r, ln_g, ln_b, out):
                 )
 
         def quantise(q):
-            codes = work.tile([P, 2, PAIR, P], U32, name="codes", align_bytes=64)
-            scales = work.tile([P, 2, PAIR, P], U8, name="scales", align_bytes=64)
+            codes = work.tile([P, OPERANDS, PAIR, P], U32, name="codes", align_bytes=64)
+            scales = work.tile([P, OPERANDS, PAIR, P], U8, name="scales", align_bytes=64)
             nc.vector.quantize_mx(
                 out=codes[:].rearrange("p x j r -> p (x j r)").bitcast(FP8X4),
                 scales=scales[:].rearrange("p x j r -> p (x j r)"),
@@ -296,10 +323,10 @@ def tile_gnnnicheencoder_pa_t_kernel(tc, h, W_l, b_l, W_r, ln_g, ln_b, out):
         def to_features(q):
             normal = kept[("normal", q)]
             banks = []
-            for half in range(CHUNKS // 2):
-                normal_turned = features_pool.tile([P, 2, PAIR, P], F32)
-                for x in range(2):
-                    f = 2 * half + x
+            for bank in range(CHUNKS // CHUNKS_PER_BANK):
+                normal_turned = features_pool.tile([P, CHUNKS_PER_BANK, PAIR, P], F32)
+                for x in range(CHUNKS_PER_BANK):
+                    f = CHUNKS_PER_BANK * bank + x
                     for j in range(PAIR):
                         nc.tensor.transpose(
                             normal_turned[:, x, j, :], normal[:, j, f * P : (f + 1) * P], identity[:]
@@ -311,7 +338,8 @@ def tile_gnnnicheencoder_pa_t_kernel(tc, h, W_l, b_l, W_r, ln_g, ln_b, out):
             bent = work.tile([P, CHUNKS, PAIR, P], F32, name="bent")
             straight = work.tile([P, CHUNKS, PAIR, P], F32, name="straight")
             for f in range(CHUNKS):
-                normal_turned = kept[("normal_turned", q)][f // 2][:, f % 2, :, :]
+                banks = kept[("normal_turned", q)]
+                normal_turned = banks[f // CHUNKS_PER_BANK][:, f % CHUNKS_PER_BANK, :, :]
                 nc.scalar.activation(
                     out=bent[:, f, :, :],
                     in_=normal_turned,
@@ -362,9 +390,9 @@ def tile_gnnnicheencoder_pa_t_kernel(tc, h, W_l, b_l, W_r, ln_g, ln_b, out):
                 )
                 nc.sync.dma_start(out=out[s * P : (s + 1) * P, i, :], in_=result[:])
 
-        def run(stage_of_pair, q):
+        def run(station, q):
             if 0 <= q < count:
-                stage_of_pair(q)
+                station(q)
 
         sum_nodes_of_first_block()
 
@@ -379,30 +407,30 @@ def tile_gnnnicheencoder_pa_t_kernel(tc, h, W_l, b_l, W_r, ln_g, ln_b, out):
         line_term = const.tile([P, 2 * CHUNKS], F32)
         nc.vector.tensor_scalar_mul(out=line_term[:], in0=per_feature[:], scalar1=LEAKY_SLOPE)
 
-        for k in range(count + DEPTH):
+        for k in range(count + AT_RESIDUAL):
             for s in range(1, BLOCKS):
-                since = k - pair_of_last[s - 1]
+                since = k - first_pair[s - 1]
                 if 0 <= since < GRAPHS_PER_SUM // LOADS_PER_STEP:
                     for g in range(LOADS_PER_STEP * since, LOADS_PER_STEP * (since + 1)):
                         load_nodes(s, g)
                 if since == GRAPHS_PER_SUM // LOADS_PER_STEP:
                     load_graphs(s)
-            run(add_residual, k - 9)
-            run(add_bias, k - 4)
-            run(normalise, k - 6)
-            run(negate_mean, k - 5)
-            run(group, k - 1)
-            run(to_features, k - 7)
-            run(to_rows, k - 8)
-            run(turn, k)
+            run(add_residual, k - AT_RESIDUAL)
+            run(add_bias, k - AT_BIAS)
+            run(normalise, k - AT_NORMALISE)
+            run(negate_mean, k - AT_STATISTICS)
+            run(group, k - AT_GROUP)
+            run(to_features, k - AT_FEATURES)
+            run(to_rows, k - AT_ROWS)
+            run(turn, k - AT_TURN)
             for s in range(1, BLOCKS):
-                first = pair_of_last[s] + 1 - SUMS // SUMS_PER_STEP
+                first = first_pair[s] + 1 - SUMS // SUMS_PER_STEP
                 if first <= k < first + SUMS // SUMS_PER_STEP:
                     for T in range(SUMS_PER_STEP * (k - first), SUMS_PER_STEP * (k - first + 1)):
                         sum_nodes(s, T)
-            run(multiply, k - 3)
-            run(sum_squares, k - 5)
-            run(two_terms, k - 7)
-            run(invert_deviation, k - 5)
-            run(quantise, k - 2)
-            run(neighbours, k - 1)
+            run(multiply, k - AT_MULTIPLY)
+            run(sum_squares, k - AT_STATISTICS)
+            run(two_terms, k - AT_FEATURES)
+            run(invert_deviation, k - AT_STATISTICS)
+            run(quantise, k - AT_QUANTISE)
+            run(neighbours, k - AT_GROUP)

from contextlib import ExitStack

import concourse.mybir as mybir
from concourse.masks import make_identity

F32 = mybir.dt.float32
BF16 = mybir.dt.bfloat16
I32 = mybir.dt.int32
U32 = mybir.dt.uint32
U8 = mybir.dt.uint8
FP8X4 = mybir.dt.float8_e4m3fn_x4
ALU = mybir.AluOpType
ACT = mybir.ActivationFunctionType
AXIS = mybir.AxisListType

P = 128
PACK = 4
WORD = 2
HALVES = 2
GRAPHS = 512
NODES = 17
D = 512
CHUNKS = D // P
CHUNKS_PER_BANK = 2
BLOCKS = GRAPHS // P
OTHERS = NODES - 1
LAST = NODES - 1
GRAPHS_PER_SUM = P // OTHERS
SUMS = P // GRAPHS_PER_SUM
LN_EPS = 1e-5
LEAKY_SLOPE = 0.01
PAIR = 2
OPERANDS = 2
SUMS_PER_STEP = 4
LOADS_PER_STEP = 2
NODES_PER_LOAD = 4

AT_TURN = 0
AT_GROUP = 1
AT_QUANTISE = 2
AT_MULTIPLY = 3
AT_BIAS = 4
AT_STATISTICS = 5
AT_NORMALISE = 6
AT_FEATURES = 7
AT_ROWS = 8
AT_RESIDUAL = 9

FLOPS = 2 * 2 * GRAPHS * NODES * D * D


def turn_words(nc, identity, rows, turned):
    words = rows.bitcast(F32)
    for u in range(HALVES):
        nc.tensor.transpose(turned[:, u, :], words[:, u * P : (u + 1) * P], identity[:])


def group_words(nc, turned, grouped):
    nc.scalar.copy(out=grouped.bitcast(F32), in_=turned[:].rearrange("p j u r -> p j r u"))


def quantise_weight(nc, staging, turned_pool, identity, weight, codes, scales):
    rows = staging.tile([P, CHUNKS, D], BF16, name="weight_rows")
    nc.sync.dma_start(out=rows[:], in_=weight.rearrange("(a p) k -> p a k", p=P))
    grouped = staging.tile([P, D, PACK], BF16, name="weight_grouped", align_bytes=64)
    for a in range(0, CHUNKS, PAIR):
        turned = turned_pool.tile([P, PAIR, HALVES, P], F32)
        for j in range(PAIR):
            turn_words(nc, identity, rows[:, a + j, :], turned[:, j, :, :])
        group_words(
            nc, turned, grouped[:, a * P : (a + PAIR) * P, :].rearrange("p (j o) t -> p j o t", j=PAIR)
        )
    nc.vector.quantize_mx(
        out=codes[:].bitcast(FP8X4),
        scales=scales[:],
        in_=grouped[:].rearrange("p o t -> p (o t)"),
    )


def tile_gnnnicheencoder_pa_t_kernel(tc, h, W_l, b_l, W_r, ln_g, ln_b, out):
    nc = tc.nc
    with ExitStack() as stack:
        stack.enter_context(tc.manual_schedule())
        const = stack.enter_context(tc.tile_pool(name="const", bufs=1))
        staging = stack.enter_context(tc.tile_pool(name="stage", bufs=2))
        blocks = stack.enter_context(tc.tile_pool(name="blocks", bufs=BLOCKS))
        means = stack.enter_context(tc.tile_pool(name="means", bufs=2))
        work = stack.enter_context(tc.tile_pool(name="work", bufs=2))
        stats = stack.enter_context(tc.tile_pool(name="stats", bufs=4))
        turned_pool = stack.enter_context(tc.psum_pool(name="turned", bufs=1))
        sums_pool = stack.enter_context(tc.psum_pool(name="sums", bufs=1))
        acc_pool = stack.enter_context(tc.psum_pool(name="acc", bufs=PAIR))
        features_pool = stack.enter_context(tc.psum_pool(name="features", bufs=PAIR))
        rows_pool = stack.enter_context(tc.psum_pool(name="rows", bufs=PAIR))

        identity = const.tile([P, P], F32)
        make_identity(nc, identity[:])
        graph_of_partition = const.tile([P, GRAPHS_PER_SUM], F32)
        nc.vector.tensor_reduce(
            out=graph_of_partition[:],
            in_=identity[:].rearrange("p (i g) -> p g i", g=GRAPHS_PER_SUM),
            axis=AXIS.X,
            op=ALU.add,
        )
        node_sum = const.tile([P, GRAPHS_PER_SUM], BF16)
        nc.vector.tensor_scalar_mul(out=node_sum[:], in0=graph_of_partition[:], scalar1=1.0 / OTHERS)
        sixteenth = const.tile([P, P], BF16)
        nc.vector.tensor_scalar_mul(out=sixteenth[:], in0=identity[:], scalar1=1.0 / OTHERS)
        eps = const.tile([P, 1], F32)
        nc.vector.memset(eps[:], LN_EPS)
        first_function = const.tile([P, 1], F32)
        nc.scalar.activation(out=first_function[:], in_=eps[:], func=ACT.Abs_reciprocal_sqrt)
        vector_rows = const.tile([P, P], BF16)
        nc.vector.memset(vector_rows[:].bitcast(I32), 0)

        wr_codes = const.tile([P, D], U32, align_bytes=64)
        wr_scales = const.tile([P, D], U8, align_bytes=64)
        wl_codes = const.tile([P, D], U32, align_bytes=64)
        wl_scales = const.tile([P, D], U8, align_bytes=64)
        quantise_weight(nc, staging, turned_pool, identity, W_r, wr_codes, wr_scales)
        quantise_weight(nc, staging, turned_pool, identity, W_l, wl_codes, wl_scales)

        by_graph = {}
        by_node = {}

        def load_graphs(s):
            block = h[s * P : (s + 1) * P, :, :]
            by_graph[s] = blocks.tile([P, NODES, D], BF16, name="by_graph")
            nc.sync.dma_start(out=by_graph[s][:, LAST, :], in_=block[:, LAST, :])
            for i in range(0, LAST, NODES_PER_LOAD):
                nc.sync.dma_start(
                    out=by_graph[s][:, i : i + NODES_PER_LOAD, :], in_=block[:, i : i + NODES_PER_LOAD, :]
                )

        def load_nodes(s, g):
            if g == 0:
                by_node[s] = blocks.tile([P, SUMS, D], BF16, name="by_node", bufs=2)
            spread = h[s * P : (s + 1) * P, 0:LAST, :].rearrange(
                "(T g) i k -> g i T k", g=GRAPHS_PER_SUM
            )
            nc.sync.dma_start(out=by_node[s][g:P:GRAPHS_PER_SUM, :, :], in_=spread[g])

        load_graphs(0)
        bias_rows = const.tile([P, D], BF16)
        nc.sync.dma_start(out=bias_rows[:], in_=b_l.partition_broadcast(P))
        nc.sync.dma_start(out=vector_rows[0:CHUNKS, :], in_=ln_g.rearrange("(f p) -> f p", p=P))
        nc.sync.dma_start(
            out=vector_rows[CHUNKS : 2 * CHUNKS, :], in_=ln_b.rearrange("(f p) -> f p", p=P)
        )

        tiles = [(s, i) for s in range(BLOCKS) for i in [LAST] + list(range(LAST))]
        count = len(tiles) // PAIR
        first_pair = [s * NODES // PAIR for s in range(BLOCKS)]
        sums_of = {}
        mean_of = {}
        kept = {}

        def sum_nodes(s, T):
            if T == 0:
                sums_of[s] = sums_pool.tile([P, PACK, P], F32, name="sums")
            columns = by_node[s][:, T, :].rearrange("p (u q e) -> p u e q", u=HALVES, e=WORD)
            for t in range(PACK):
                nc.tensor.matmul(
                    out=sums_of[s][:, t, T * GRAPHS_PER_SUM : (T + 1) * GRAPHS_PER_SUM],
                    lhsT=columns[:, t // WORD, t % WORD, :],
                    rhs=node_sum[:],
                    start=True,
                    stop=True,
                )

        def sum_nodes_of_first_block():
            total = acc_pool.tile([P, D], F32, name="acc")
            for i in range(LAST):
                nc.tensor.matmul(
                    out=total[:],
                    lhsT=sixteenth[:],
                    rhs=by_graph[0][:, i, :],
                    start=(i == 0),
                    stop=(i == LAST - 1),
                )
            total_rows = const.tile([P, D], F32)
            nc.scalar.copy(out=total_rows[:], in_=total[:])
            sums_of[0] = sums_pool.tile([P, PACK, P], F32, name="sums")
            columns = total_rows[:].rearrange("p (u q e) -> p u e q", u=HALVES, e=WORD)
            for t in range(PACK):
                nc.tensor.transpose(
                    sums_of[0][:, t, :], columns[:, t // WORD, t % WORD, :], identity[:]
                )

        def turn(q):
            turned = turned_pool.tile([P, PAIR, HALVES, P], F32)
            for j in range(PAIR):
                s, i = tiles[PAIR * q + j]
                turn_words(nc, identity, by_graph[s][:, i, :], turned[:, j, :, :])
            kept[("turned", q)] = turned

        def group(q):
            grouped = work.tile(
                [P, OPERANDS, PAIR, P, PACK], BF16, name="grouped", align_bytes=64, bufs=3
            )
            group_words(nc, kept[("turned", q)], grouped[:, 0, :, :, :])
            kept[("grouped", q)] = grouped

        def neighbours(q):
            grouped = kept[("grouped", q)]
            for j in range(PAIR):
                s, i = tiles[PAIR * q + j]
                if i == LAST:
                    mean = means.tile([P, P, PACK], F32, name="mean")
                    nc.vector.scalar_tensor_tensor(
                        out=mean[:],
                        in0=grouped[:, 0, j, :, :],
                        scalar=1.0 / OTHERS,
                        in1=sums_of[s][:].rearrange("p t g -> p g t"),
                        op0=ALU.mult,
                        op1=ALU.add,
                    )
                    mean_of[s] = mean
                nc.vector.scalar_tensor_tensor(
                    out=grouped[:, 1, j, :, :],
                    in0=grouped[:, 0, j, :, :],
                    scalar=-1.0 / OTHERS,
                    in1=mean_of[s][:],
                    op0=ALU.mult,
                    op1=ALU.add,
                )

        def quantise(q):
            codes = work.tile([P, OPERANDS, PAIR, P], U32, name="codes", align_bytes=64)
            scales = work.tile([P, OPERANDS, PAIR, P], U8, name="scales", align_bytes=64)
            nc.vector.quantize_mx(
                out=codes[:].rearrange("p x j r -> p (x j r)").bitcast(FP8X4),
                scales=scales[:].rearrange("p x j r -> p (x j r)"),
                in_=kept[("grouped", q)][:].rearrange("p x j r t -> p (x j r t)"),
            )
            kept[("codes", q)] = (codes, scales)

        def multiply(q):
            codes, scales = kept[("codes", q)]
            banks = []
            for j in range(PAIR):
                acc = acc_pool.tile([P, D], F32)
                nc.tensor.matmul_mx(
                    out=acc[:],
                    lhsT=codes[:, 0, j, :].bitcast(FP8X4),
                    lhsT_scale=scales[:, 0, j, :],
                    rhs=wr_codes[:].bitcast(FP8X4),
                    rhs_scale=wr_scales[:],
                    start=True,
                    stop=False,
                )
                nc.tensor.matmul_mx(
                    out=acc[:],
                    lhsT=codes[:, 1, j, :].bitcast(FP8X4),
                    lhsT_scale=scales[:, 1, j, :],
                    rhs=wl_codes[:].bitcast(FP8X4),
                    rhs_scale=wl_scales[:],
                    start=False,
                    stop=True,
                )
                banks.append(acc)
            kept[("acc", q)] = banks

        def add_bias(q):
            c = work.tile([P, PAIR, D], F32, name="c", bufs=3)
            row_sum = stats.tile([P, PAIR], F32, name="row_sum")
            for j in range(PAIR):
                nc.vector.scalar_tensor_tensor(
                    out=c[:, j, :],
                    in0=kept[("acc", q)][j][:],
                    scalar=1.0,
                    in1=bias_rows[:],
                    op0=ALU.mult,
                    op1=ALU.add,
                    accum_out=row_sum[:, j : j + 1],
                )
            kept[("c", q)] = c
            kept[("row_sum", q)] = row_sum

        def negate_mean(q):
            minus_mean = stats.tile([P, PAIR], F32, name="minus_mean")
            nc.scalar.mul(out=minus_mean[:], in_=kept[("row_sum", q)][:], mul=-1.0 / D)
            kept[("minus_mean", q)] = minus_mean

        def sum_squares(q):
            square_sum = stats.tile([P, PAIR], F32, name="square_sum")
            for j in range(PAIR):
                squares = work.tile([P, D], BF16, name="squares")
                nc.scalar.activation(
                    out=squares[:],
                    in_=kept[("c", q)][:, j, :],
                    func=ACT.Square,
                    bias=kept[("minus_mean", q)][:, j : j + 1],
                    scale=1.0,
                    accum_out=square_sum[:, j : j + 1],
                )
            kept[("square_sum", q)] = square_sum

        def invert_deviation(q):
            inverse = stats.tile([P, PAIR], F32, name="inverse")
            nc.scalar.activation(
                out=inverse[:],
                in_=kept[("square_sum", q)][:],
                func=ACT.Abs_reciprocal_sqrt,
                bias=eps[:],
                scale=1.0 / D,
            )
            kept[("inverse", q)] = inverse

        def normalise(q):
            normal = work.tile([P, PAIR, D], F32, name="normal")
            for j in range(PAIR):
                nc.gpsimd.tensor_scalar(
                    out=normal[:, j, :],
                    in0=kept[("c", q)][:, j, :],
                    scalar1=kept[("minus_mean", q)][:, j : j + 1],
                    scalar2=kept[("inverse", q)][:, j : j + 1],
                    op0=ALU.add,
                    op1=ALU.mult,
                )
            kept[("normal", q)] = normal

        def to_features(q):
            normal = kept[("normal", q)]
            banks = []
            for bank in range(CHUNKS // CHUNKS_PER_BANK):
                normal_turned = features_pool.tile([P, CHUNKS_PER_BANK, PAIR, P], F32)
                for x in range(CHUNKS_PER_BANK):
                    f = CHUNKS_PER_BANK * bank + x
                    for j in range(PAIR):
                        nc.tensor.transpose(
                            normal_turned[:, x, j, :], normal[:, j, f * P : (f + 1) * P], identity[:]
                        )
                banks.append(normal_turned)
            kept[("normal_turned", q)] = banks

        def two_terms(q):
            bent = work.tile([P, CHUNKS, PAIR, P], F32, name="bent")
            straight = work.tile([P, CHUNKS, PAIR, P], F32, name="straight")
            for f in range(CHUNKS):
                banks = kept[("normal_turned", q)]
                normal_turned = banks[f // CHUNKS_PER_BANK][:, f % CHUNKS_PER_BANK, :, :]
                nc.scalar.activation(
                    out=bent[:, f, :, :],
                    in_=normal_turned,
                    func=ACT.Relu,
                    bias=relu_term[:, CHUNKS + f : CHUNKS + f + 1],
                    scale=relu_term[:, f : f + 1],
                )
                nc.scalar.activation(
                    out=straight[:, f, :, :],
                    in_=normal_turned,
                    func=ACT.Identity,
                    bias=line_term[:, CHUNKS + f : CHUNKS + f + 1],
                    scale=line_term[:, f : f + 1],
                )
            kept[("terms", q)] = (bent, straight)

        def to_rows(q):
            bent, straight = kept[("terms", q)]
            banks = []
            for j in range(PAIR):
                a_rows = rows_pool.tile([P, D], F32)
                for f in range(CHUNKS):
                    nc.tensor.matmul(
                        out=a_rows[:, f * P : (f + 1) * P],
                        lhsT=bent[:, f, j, :],
                        rhs=identity[:],
                        is_transpose=True,
                        start=True,
                        stop=False,
                    )
                    nc.tensor.matmul(
                        out=a_rows[:, f * P : (f + 1) * P],
                        lhsT=straight[:, f, j, :],
                        rhs=identity[:],
                        is_transpose=True,
                        start=False,
                        stop=True,
                    )
                banks.append(a_rows)
            kept[("a_rows", q)] = banks

        def add_residual(q):
            for j in range(PAIR):
                s, i = tiles[PAIR * q + j]
                result = work.tile([P, D], F32, name="result", bufs=4)
                nc.vector.tensor_add(
                    out=result[:], in0=kept[("a_rows", q)][j][:], in1=by_graph[s][:, i, :]
                )
                nc.sync.dma_start(out=out[s * P : (s + 1) * P, i, :], in_=result[:])

        def run(station, q):
            if 0 <= q < count:
                station(q)

        sum_nodes_of_first_block()

        vector_rows_f32 = const.tile([P, P], F32)
        nc.vector.tensor_copy(out=vector_rows_f32[:], in_=vector_rows[:])
        turned = turned_pool.tile([P, PAIR, HALVES, P], F32)
        nc.tensor.transpose(turned[:, 0, 0, :], vector_rows_f32[:], identity[:])
        per_feature = const.tile([P, 2 * CHUNKS], F32)
        nc.vector.tensor_copy(out=per_feature[:], in_=turned[:, 0, 0, 0 : 2 * CHUNKS])
        relu_term = const.tile([P, 2 * CHUNKS], F32)
        nc.vector.tensor_scalar_mul(out=relu_term[:], in0=per_feature[:], scalar1=1.0 - LEAKY_SLOPE)
        line_term = const.tile([P, 2 * CHUNKS], F32)
        nc.vector.tensor_scalar_mul(out=line_term[:], in0=per_feature[:], scalar1=LEAKY_SLOPE)

        for k in range(count + AT_RESIDUAL):
            for s in range(1, BLOCKS):
                since = k - first_pair[s - 1]
                if 0 <= since < GRAPHS_PER_SUM // LOADS_PER_STEP:
                    for g in range(LOADS_PER_STEP * since, LOADS_PER_STEP * (since + 1)):
                        load_nodes(s, g)
                if since == GRAPHS_PER_SUM // LOADS_PER_STEP:
                    load_graphs(s)
            run(add_residual, k - AT_RESIDUAL)
            run(add_bias, k - AT_BIAS)
            run(normalise, k - AT_NORMALISE)
            run(negate_mean, k - AT_STATISTICS)
            run(group, k - AT_GROUP)
            run(to_features, k - AT_FEATURES)
            run(to_rows, k - AT_ROWS)
            run(turn, k - AT_TURN)
            for s in range(1, BLOCKS):
                first = first_pair[s] + 1 - SUMS // SUMS_PER_STEP
                if first <= k < first + SUMS // SUMS_PER_STEP:
                    for T in range(SUMS_PER_STEP * (k - first), SUMS_PER_STEP * (k - first + 1)):
                        sum_nodes(s, T)
            run(multiply, k - AT_MULTIPLY)
            run(sum_squares, k - AT_STATISTICS)
            run(two_terms, k - AT_FEATURES)
            run(invert_deviation, k - AT_STATISTICS)
            run(quantise, k - AT_QUANTISE)
            run(neighbours, k - AT_GROUP)
